import numpy as np
import ml_dtypes


def mxq(x, axis, fmt="e4m3"):
    dtype, down = {"e4m3": (ml_dtypes.float8_e4m3fn, 7), "e5m2": (ml_dtypes.float8_e5m2, 14)}[fmt]
    v = np.moveaxis(np.asarray(x, np.float32).astype(ml_dtypes.bfloat16).astype(np.float64), axis, -1)
    blocks = v.reshape(v.shape[:-1] + (-1, 32))
    amax = np.abs(blocks).max(-1, keepdims=True)
    byte = np.maximum(np.where(amax > 0, np.frexp(amax)[1] - 1 + 127, 0) - down, 1)
    scale = np.exp2(byte - 127.0)
    codes = (blocks / scale).astype(np.float32).astype(dtype).astype(np.float64)
    return np.moveaxis((codes * scale).reshape(v.shape), -1, axis)


WIDE = False


def mx_kscale(k):
    if not WIDE:
        return np.ones(k)
    levels = np.array([10, -10, 5, -5, 0])
    a = np.random.permutation(np.resize(levels, k // 512 * 4)).reshape(k // 512, 4)
    idx = np.arange(k)
    return np.exp2(a[idx // 512, idx % 128 // 32])


BF16 = ml_dtypes.bfloat16


def bf(x):
    return np.asarray(x, np.float32).astype(BF16)


def f64(x):
    return np.asarray(x).astype(np.float64)


M, K, N = 128, 1024, 1024


def ternary_quantize(w):
    alpha = np.mean(np.abs(w))
    threshold = 0.7 * alpha
    w_ternary = np.where(np.abs(w) < threshold, np.zeros_like(w), np.sign(w))
    return alpha * w_ternary


def setup_inputs():
    s = mx_kscale(K)
    c = 1.0 / (np.mean(1.0 / s) * np.min(s))
    return {"x": bf(np.random.standard_normal((M, K)) * s),
            "w": bf(np.random.uniform(-1.0, 1.0, (K, N)) * 4.5 / np.sqrt(K) * c / s[:, None]),
            "b": bf(np.random.standard_normal(N) * 0.5)}


def reference(x, w, b):
    wt = ternary_quantize(f64(w))
    return (mxq(f64(x), 1, "e4m3") @ mxq(wt, 0, "e4m3")) + f64(b)

@@ -1,0 +1,183 @@
+from contextlib import ExitStack
+
+import concourse.mybir as mybir
+from concourse.masks import make_identity
+
+BF16 = mybir.dt.bfloat16
+F32 = mybir.dt.float32
+U32 = mybir.dt.uint32
+U8 = mybir.dt.uint8
+FP8X4 = mybir.dt.float8_e4m3fn_x4
+ALU = mybir.AluOpType
+ACT = mybir.ActivationFunctionType
+AXIS_X = mybir.AxisListType.X
+
+P = 128
+PACK = 4
+M, K, N = 128, 1024, 1024
+PASSES = K // (P * PACK)
+SLABS = K // P
+N_TILE = 512
+N_TILES = N // N_TILE
+HALF = N // 2
+THRESHOLD_FACTOR = 0.7
+
+FLOPS = 2 * M * K * N
+
+
+def tile_ternarydense_s_kernel(tc, x, w, b, out):
+    nc = tc.nc
+    with ExitStack() as stack:
+        keep = stack.enter_context(tc.tile_pool(name="keep", bufs=1))
+        work = stack.enter_context(tc.tile_pool(name="work", bufs=2))
+        psum = stack.enter_context(tc.psum_pool(name="psum", bufs=1))
+        stack.enter_context(tc.manual_schedule())
+
+        ones = keep.tile([P, P], F32)
+        nc.vector.memset(ones[:], 1.0)
+        ident = keep.tile([P, P], BF16)
+        make_identity(nc, ident[:])
+
+        w_sb = keep.tile([P, SLABS, N], BF16)
+        for r in range(SLABS):
+            nc.sync.dma_start(out=w_sb[:, r, :], in_=w[r * P : (r + 1) * P, :])
+        x_sb = keep.tile([P, K], BF16)
+        nc.sync.dma_start(out=x_sb[:], in_=x)
+        bias_all = keep.tile([P, N], BF16)
+        nc.sync.dma_start(out=bias_all[:], in_=b.partition_broadcast(P))
+
+        slab_sums = keep.tile([P, 2 * SLABS], F32)
+        v_abs = keep.tile([P, SLABS, HALF], BF16)
+        s_abs = keep.tile([P, SLABS, N - HALF], BF16)
+        for r in range(SLABS):
+            nc.vector.scalar_tensor_tensor(
+                out=v_abs[:, r, :],
+                in0=w_sb[:, r, 0:HALF],
+                scalar=-1.0,
+                in1=w_sb[:, r, 0:HALF],
+                op0=ALU.mult,
+                op1=ALU.max,
+                accum_out=slab_sums[:, r : r + 1],
+            )
+            nc.scalar.activation(
+                out=s_abs[:, r, :],
+                in_=w_sb[:, r, HALF:N],
+                func=ACT.Abs,
+                accum_out=slab_sums[:, SLABS + r : SLABS + r + 1],
+            )
+        row_sum = keep.tile([P, 1], F32)
+        nc.vector.tensor_reduce(out=row_sum[:], in_=slab_sums[:], axis=AXIS_X, op=ALU.add)
+        total = psum.tile([P, 1], F32)
+        nc.tensor.matmul(out=total[:], lhsT=ones[:], rhs=row_sum[:], start=True, stop=True)
+
+        units = [(g, j) for g in range(PASSES) for j in range(N_TILES)]
+        w_grouped = [
+            keep.tile([P, N_TILE, PACK], BF16, name="w_grouped_%d" % u) for u in range(len(units))
+        ]
+
+        def regroup(copy, u, first, count):
+            g, j = units[u]
+            slabs = w_sb[:, g * PACK : (g + 1) * PACK, j * N_TILE + first : j * N_TILE + first + count]
+            copy(
+                out=w_grouped[u][:, first : first + count, :].rearrange("p (c i) t -> p c t i", i=4),
+                in_=slabs.rearrange("p t (c i) -> p c t i", i=4),
+            )
+
+        regroup(nc.scalar.copy, 0, 0, N_TILE // 2)
+        regroup(nc.vector.tensor_copy, 0, N_TILE // 2, N_TILE // 2)
+
+        alpha = keep.tile([P, 1], F32)
+        thr = keep.tile([P, 1], F32)
+        neg_thr = keep.tile([P, 1], F32)
+        mean = 1.0 / (K * N)
+        nc.vector.tensor_scalar(
+            out=alpha[:], in0=total[:], scalar1=mean, scalar2=None, op0=ALU.mult
+        )
+        nc.vector.tensor_scalar(
+            out=thr[:],
+            in0=total[:],
+            scalar1=mean,
+            scalar2=THRESHOLD_FACTOR,
+            op0=ALU.mult,
+            op1=ALU.mult,
+        )
+        nc.vector.tensor_scalar(
+            out=neg_thr[:],
+            in0=total[:],
+            scalar1=mean,
+            scalar2=-THRESHOLD_FACTOR,
+            op0=ALU.mult,
+            op1=ALU.mult,
+        )
+
+        x_t = psum.tile([P, SLABS, M], BF16)
+        for r in range(SLABS):
+            nc.tensor.transpose(x_t[:, r, :], x_sb[:, r * P : (r + 1) * P], ident[:])
+        x_grouped = keep.tile([P, PASSES, M, PACK], BF16, align_bytes=64)
+
+        regroup(nc.scalar.copy, 1, 0, N_TILE)
+        nc.scalar.copy(out=x_grouped[:], in_=x_t[:].rearrange("p (g t) m -> p g m t", t=PACK))
+        for u in range(2, len(units)):
+            regroup(nc.scalar.copy, u, 0, N_TILE)
+
+        x_codes = keep.tile([P, PASSES, M], U32, align_bytes=64)
+        x_scales = keep.tile([P, PASSES, M], U8, align_bytes=64)
+        w_codes = keep.tile([P, PASSES, N], U32, align_bytes=64)
+        w_scales = keep.tile([P, PASSES, N], U8, align_bytes=64)
+        acc = [psum.tile([P, N_TILE], F32, name="acc_%d" % j) for j in range(N_TILES)]
+        out_sb = keep.tile([P, N], F32)
+        pos = [work.tile([P, N_TILE * PACK], BF16, name="pos", tag="pos") for u in units]
+        neg = [work.tile([P, N_TILE * PACK], BF16, name="neg", tag="neg") for u in units]
+        wt = [
+            work.tile([P, N_TILE * PACK], BF16, name="wt", tag="wt", align_bytes=64) for u in units
+        ]
+
+        def compare(u):
+            flat = w_grouped[u][:].rearrange("p n t -> p (n t)")
+            nc.vector.tensor_scalar(
+                out=pos[u][:], in0=flat, scalar1=thr[:], scalar2=alpha[:], op0=ALU.is_ge, op1=ALU.mult
+            )
+            nc.vector.tensor_scalar(
+                out=neg[u][:],
+                in0=flat,
+                scalar1=neg_thr[:],
+                scalar2=alpha[:],
+                op0=ALU.is_le,
+                op1=ALU.mult,
+            )
+
+        def add_bias_and_store(j):
+            cols = slice(j * N_TILE, (j + 1) * N_TILE)
+            nc.vector.tensor_tensor(
+                out=out_sb[:, cols], in0=acc[j][:], in1=bias_all[:, cols], op=ALU.add
+            )
+            nc.sync.dma_start(out=out[:, cols], in_=out_sb[:, cols])
+
+        compare(0)
+        for u in range(len(units)):
+            g, j = units[u]
+            cols = slice(j * N_TILE, (j + 1) * N_TILE)
+            nc.vector.tensor_tensor(out=wt[u][:], in0=pos[u][:], in1=neg[u][:], op=ALU.subtract)
+            if u + 1 < len(units):
+                compare(u + 1)
+            if u == 0:
+                nc.vector.quantize_mx(
+                    out=x_codes[:].rearrange("p g m -> p (g m)").bitcast(FP8X4),
+                    scales=x_scales[:].rearrange("p g m -> p (g m)"),
+                    in_=x_grouped[:].rearrange("p g m t -> p (g m t)"),
+                )
+            if g == PASSES - 1 and j > 0:
+                add_bias_and_store(j - 1)
+            nc.vector.quantize_mx(
+                out=w_codes[:, g, cols].bitcast(FP8X4), scales=w_scales[:, g, cols], in_=wt[u][:]
+            )
+            nc.tensor.matmul_mx(
+                out=acc[j][:],
+                lhsT=x_codes[:, g, :].bitcast(FP8X4),
+                lhsT_scale=x_scales[:, g, :],
+                rhs=w_codes[:, g, cols].bitcast(FP8X4),
+                rhs_scale=w_scales[:, g, cols],
+                start=(g == 0),
+                stop=(g == PASSES - 1),
+            )
+        add_bias_and_store(N_TILES - 1)

@@ -19,6 +19,7 @@ PASSES = K // (P * PACK)
 SLABS = K // P
 N_TILE = 512
 N_TILES = N // N_TILE
+COLUMN_GROUPS = [[(0, 512)], [(512, 256), (768, 256)]]
 HALF = N // 2
 THRESHOLD_FACTOR = 0.7
 
@@ -37,6 +38,10 @@ def tile_ternarydense_s_kernel(tc, x, w, b, out):
         nc.vector.memset(ones[:], 1.0)
         ident = keep.tile([P, P], BF16)
         make_identity(nc, ident[:])
+        mean = 1.0 / (K * N)
+        factors = keep.tile([P, 3], F32)
+        for i, factor in enumerate((mean, THRESHOLD_FACTOR * mean, -THRESHOLD_FACTOR * mean)):
+            nc.vector.memset(factors[:, i : i + 1], factor)
 
         w_sb = keep.tile([P, SLABS, N], BF16)
         for r in range(SLABS):
@@ -86,29 +91,13 @@ def tile_ternarydense_s_kernel(tc, x, w, b, out):
         regroup(nc.scalar.copy, 0, 0, N_TILE // 2)
         regroup(nc.vector.tensor_copy, 0, N_TILE // 2, N_TILE // 2)
 
-        alpha = keep.tile([P, 1], F32)
-        thr = keep.tile([P, 1], F32)
-        neg_thr = keep.tile([P, 1], F32)
-        mean = 1.0 / (K * N)
-        nc.vector.tensor_scalar(
-            out=alpha[:], in0=total[:], scalar1=mean, scalar2=None, op0=ALU.mult
+        levels = keep.tile([P, 3], F32)
+        nc.vector.tensor_tensor(
+            out=levels[:], in0=total[:].to_broadcast([P, 3]), in1=factors[:], op=ALU.mult
         )
-        nc.vector.tensor_scalar(
-            out=thr[:],
-            in0=total[:],
-            scalar1=mean,
-            scalar2=THRESHOLD_FACTOR,
-            op0=ALU.mult,
-            op1=ALU.mult,
-        )
-        nc.vector.tensor_scalar(
-            out=neg_thr[:],
-            in0=total[:],
-            scalar1=mean,
-            scalar2=-THRESHOLD_FACTOR,
-            op0=ALU.mult,
-            op1=ALU.mult,
-        )
+        alpha = levels[:, 0:1]
+        thr = levels[:, 1:2]
+        neg_thr = levels[:, 2:3]
 
         x_t = psum.tile([P, SLABS, M], BF16)
         for r in range(SLABS):
@@ -124,7 +113,11 @@ def tile_ternarydense_s_kernel(tc, x, w, b, out):
         x_scales = keep.tile([P, PASSES, M], U8, align_bytes=64)
         w_codes = keep.tile([P, PASSES, N], U32, align_bytes=64)
         w_scales = keep.tile([P, PASSES, N], U8, align_bytes=64)
-        acc = [psum.tile([P, N_TILE], F32, name="acc_%d" % j) for j in range(N_TILES)]
+        acc = {
+            first: psum.tile([P, count], F32, name="acc_%d" % first)
+            for groups in COLUMN_GROUPS
+            for first, count in groups
+        }
         out_sb = keep.tile([P, N], F32)
         pos = [work.tile([P, N_TILE * PACK], BF16, name="pos", tag="pos") for u in units]
         neg = [work.tile([P, N_TILE * PACK], BF16, name="neg", tag="neg") for u in units]
@@ -135,28 +128,28 @@ def tile_ternarydense_s_kernel(tc, x, w, b, out):
         def compare(u):
             flat = w_grouped[u][:].rearrange("p n t -> p (n t)")
             nc.vector.tensor_scalar(
-                out=pos[u][:], in0=flat, scalar1=thr[:], scalar2=alpha[:], op0=ALU.is_ge, op1=ALU.mult
+                out=pos[u][:], in0=flat, scalar1=thr, scalar2=alpha, op0=ALU.is_ge, op1=ALU.mult
             )
             nc.vector.tensor_scalar(
                 out=neg[u][:],
                 in0=flat,
-                scalar1=neg_thr[:],
-                scalar2=alpha[:],
+                scalar1=neg_thr,
+                scalar2=alpha,
                 op0=ALU.is_le,
                 op1=ALU.mult,
             )
 
         def add_bias_and_store(j):
-            cols = slice(j * N_TILE, (j + 1) * N_TILE)
-            nc.vector.tensor_tensor(
-                out=out_sb[:, cols], in0=acc[j][:], in1=bias_all[:, cols], op=ALU.add
-            )
-            nc.sync.dma_start(out=out[:, cols], in_=out_sb[:, cols])
+            for first, count in COLUMN_GROUPS[j]:
+                cols = slice(first, first + count)
+                nc.vector.tensor_tensor(
+                    out=out_sb[:, cols], in0=acc[first][:], in1=bias_all[:, cols], op=ALU.add
+                )
+                nc.sync.dma_start(out=out[:, cols], in_=out_sb[:, cols])
 
         compare(0)
         for u in range(len(units)):
             g, j = units[u]
-            cols = slice(j * N_TILE, (j + 1) * N_TILE)
             nc.vector.tensor_tensor(out=wt[u][:], in0=pos[u][:], in1=neg[u][:], op=ALU.subtract)
             if u + 1 < len(units):
                 compare(u + 1)
@@ -168,16 +161,23 @@ def tile_ternarydense_s_kernel(tc, x, w, b, out):
                 )
             if g == PASSES - 1 and j > 0:
                 add_bias_and_store(j - 1)
-            nc.vector.quantize_mx(
-                out=w_codes[:, g, cols].bitcast(FP8X4), scales=w_scales[:, g, cols], in_=wt[u][:]
-            )
-            nc.tensor.matmul_mx(
-                out=acc[j][:],
-                lhsT=x_codes[:, g, :].bitcast(FP8X4),
-                lhsT_scale=x_scales[:, g, :],
-                rhs=w_codes[:, g, cols].bitcast(FP8X4),
-                rhs_scale=w_scales[:, g, cols],
-                start=(g == 0),
-                stop=(g == PASSES - 1),
-            )
+            for first, count in COLUMN_GROUPS[j]:
+                cols = slice(first, first + count)
+                in_unit = slice((first - j * N_TILE) * PACK, (first - j * N_TILE + count) * PACK)
+                nc.vector.quantize_mx(
+                    out=w_codes[:, g, cols].bitcast(FP8X4),
+                    scales=w_scales[:, g, cols],
+                    in_=wt[u][:, in_unit],
+                )
+            for first, count in COLUMN_GROUPS[j]:
+                cols = slice(first, first + count)
+                nc.tensor.matmul_mx(
+                    out=acc[first][:],
+                    lhsT=x_codes[:, g, :].bitcast(FP8X4),
+                    lhsT_scale=x_scales[:, g, :],
+                    rhs=w_codes[:, g, cols].bitcast(FP8X4),
+                    rhs_scale=w_scales[:, g, cols],
+                    start=(g == 0),
+                    stop=(g == PASSES - 1),
+                )
         add_bias_and_store(N_TILES - 1)

@@ -5,23 +5,27 @@ from concourse.masks import make_identity
 
 BF16 = mybir.dt.bfloat16
 F32 = mybir.dt.float32
+I32 = mybir.dt.int32
 U32 = mybir.dt.uint32
 U8 = mybir.dt.uint8
 FP8X4 = mybir.dt.float8_e4m3fn_x4
 ALU = mybir.AluOpType
 ACT = mybir.ActivationFunctionType
-AXIS_X = mybir.AxisListType.X
 
 P = 128
 PACK = 4
 M, K, N = 128, 1024, 1024
 PASSES = K // (P * PACK)
 SLABS = K // P
-N_TILE = 512
-N_TILES = N // N_TILE
-COLUMN_GROUPS = [[(0, 512)], [(512, 256), (768, 256)]]
-HALF = N // 2
+SIGNED_GROUPS = [(0, 128), (128, 256), (384, 256), (640, 128)]
+SIGNED = 768
+EARLY = [(768, 128), (896, 128)]
+EARLY_WIDTH = 128
 THRESHOLD_FACTOR = 0.7
+MAGNITUDE_BITS = 0x7FFF7FFF
+SIGN_BITS = 0x80008000 - (1 << 32)
+ONES_BITS = 0x3F803F80
+SCALAR_SIGN_SLABS = (0, 1, 4)
 
 FLOPS = 2 * M * K * N
 
@@ -30,12 +34,13 @@ def tile_ternarydense_s_kernel(tc, x, w, b, out):
     nc = tc.nc
     with ExitStack() as stack:
         keep = stack.enter_context(tc.tile_pool(name="keep", bufs=1))
-        work = stack.enter_context(tc.tile_pool(name="work", bufs=2))
         psum = stack.enter_context(tc.psum_pool(name="psum", bufs=1))
         stack.enter_context(tc.manual_schedule())
 
         ones = keep.tile([P, P], F32)
         nc.vector.memset(ones[:], 1.0)
+        one_col = keep.tile([P, 1], BF16)
+        nc.vector.memset(one_col[:], 1.0)
         ident = keep.tile([P, P], BF16)
         make_identity(nc, ident[:])
         mean = 1.0 / (K * N)
@@ -51,49 +56,69 @@ def tile_ternarydense_s_kernel(tc, x, w, b, out):
         bias_all = keep.tile([P, N], BF16)
         nc.sync.dma_start(out=bias_all[:], in_=b.partition_broadcast(P))
 
-        slab_sums = keep.tile([P, 2 * SLABS], F32)
-        v_abs = keep.tile([P, SLABS, HALF], BF16)
-        s_abs = keep.tile([P, SLABS, N - HALF], BF16)
+        w_abs = keep.tile([P, SLABS, N], BF16)
+        w_sign = keep.tile([P, SLABS, SIGNED], BF16)
+        sums = psum.tile([P, 2], F32)
+        partial = sums[:, 0:1]
+        total = sums[:, 1:2]
+        early = keep.tile([P, len(EARLY), PASSES, EARLY_WIDTH, PACK], BF16)
+
+        def magnitude(r):
+            nc.vector.tensor_scalar(
+                out=w_abs[:, r, :].bitcast(I32),
+                in0=w_sb[:, r, :].bitcast(I32),
+                scalar1=MAGNITUDE_BITS,
+                scalar2=None,
+                op0=ALU.bitwise_and,
+            )
+            for c in range(N // P):
+                nc.tensor.matmul(
+                    out=partial,
+                    lhsT=w_abs[:, r, c * P : (c + 1) * P],
+                    rhs=one_col[:],
+                    start=(r == 0 and c == 0),
+                    stop=(r == SLABS - 1 and c == N // P - 1),
+                )
+
+        def vector_sign(r):
+            nc.vector.tensor_scalar(
+                out=w_sign[:, r, :].bitcast(I32),
+                in0=w_sb[:, r, 0:SIGNED].bitcast(I32),
+                scalar1=SIGN_BITS,
+                scalar2=ONES_BITS,
+                op0=ALU.bitwise_and,
+                op1=ALU.bitwise_or,
+            )
+
+        def scalar_sign(r):
+            nc.scalar.activation(out=w_sign[:, r, :], in_=w_sb[:, r, 0:SIGNED], func=ACT.Sign)
+
+        def regroup(dst, src):
+            nc.scalar.copy(
+                out=dst.rearrange("p (c i) t -> p c t i", i=4),
+                in_=src.rearrange("p t (c i) -> p c t i", i=4),
+            )
+
+        def regroup_early(g):
+            for h, (first, count) in enumerate(EARLY):
+                regroup(early[:, h, g], w_sb[:, g * PACK : (g + 1) * PACK, first : first + count])
+
         for r in range(SLABS):
-            nc.vector.scalar_tensor_tensor(
-                out=v_abs[:, r, :],
-                in0=w_sb[:, r, 0:HALF],
-                scalar=-1.0,
-                in1=w_sb[:, r, 0:HALF],
-                op0=ALU.mult,
-                op1=ALU.max,
-                accum_out=slab_sums[:, r : r + 1],
-            )
-            nc.scalar.activation(
-                out=s_abs[:, r, :],
-                in_=w_sb[:, r, HALF:N],
-                func=ACT.Abs,
-                accum_out=slab_sums[:, SLABS + r : SLABS + r + 1],
-            )
-        row_sum = keep.tile([P, 1], F32)
-        nc.vector.tensor_reduce(out=row_sum[:], in_=slab_sums[:], axis=AXIS_X, op=ALU.add)
-        total = psum.tile([P, 1], F32)
-        nc.tensor.matmul(out=total[:], lhsT=ones[:], rhs=row_sum[:], start=True, stop=True)
-
-        units = [(g, j) for g in range(PASSES) for j in range(N_TILES)]
-        w_grouped = [
-            keep.tile([P, N_TILE, PACK], BF16, name="w_grouped_%d" % u) for u in range(len(units))
-        ]
-
-        def regroup(copy, u, first, count):
-            g, j = units[u]
-            slabs = w_sb[:, g * PACK : (g + 1) * PACK, j * N_TILE + first : j * N_TILE + first + count]
-            copy(
-                out=w_grouped[u][:, first : first + count, :].rearrange("p (c i) t -> p c t i", i=4),
-                in_=slabs.rearrange("p t (c i) -> p c t i", i=4),
-            )
-
-        regroup(nc.scalar.copy, 0, 0, N_TILE // 2)
-        regroup(nc.vector.tensor_copy, 0, N_TILE // 2, N_TILE // 2)
+            magnitude(r)
+            if r in SCALAR_SIGN_SLABS:
+                scalar_sign(r)
+            else:
+                vector_sign(r)
+            if r == PACK - 1:
+                regroup_early(0)
+        regroup_early(1)
+        partial_sb = keep.tile([P, 1], F32)
+        nc.vector.tensor_copy(out=partial_sb[:], in_=partial)
+        nc.tensor.matmul(out=total, lhsT=ones[:], rhs=partial_sb[:], start=True, stop=True)
 
         levels = keep.tile([P, 3], F32)
         nc.vector.tensor_tensor(
-            out=levels[:], in0=total[:].to_broadcast([P, 3]), in1=factors[:], op=ALU.mult
+            out=levels[:], in0=total.to_broadcast([P, 3]), in1=factors[:], op=ALU.mult
         )
         alpha = levels[:, 0:1]
         thr = levels[:, 1:2]
@@ -103,81 +128,106 @@ def tile_ternarydense_s_kernel(tc, x, w, b, out):
         for r in range(SLABS):
             nc.tensor.transpose(x_t[:, r, :], x_sb[:, r * P : (r + 1) * P], ident[:])
         x_grouped = keep.tile([P, PASSES, M, PACK], BF16, align_bytes=64)
-
-        regroup(nc.scalar.copy, 1, 0, N_TILE)
         nc.scalar.copy(out=x_grouped[:], in_=x_t[:].rearrange("p (g t) m -> p g m t", t=PACK))
-        for u in range(2, len(units)):
-            regroup(nc.scalar.copy, u, 0, N_TILE)
-
         x_codes = keep.tile([P, PASSES, M], U32, align_bytes=64)
         x_scales = keep.tile([P, PASSES, M], U8, align_bytes=64)
-        w_codes = keep.tile([P, PASSES, N], U32, align_bytes=64)
-        w_scales = keep.tile([P, PASSES, N], U8, align_bytes=64)
-        acc = {
-            first: psum.tile([P, count], F32, name="acc_%d" % first)
-            for groups in COLUMN_GROUPS
+
+        groups = SIGNED_GROUPS + EARLY
+        codes = [
+            keep.tile([P, PASSES, count], U32, name="codes_%d" % first, align_bytes=64)
             for first, count in groups
-        }
+        ]
+        scales = [
+            keep.tile([P, PASSES, count], U8, name="scales_%d" % first, align_bytes=64)
+            for first, count in groups
+        ]
+        acc = [psum.tile([P, count], F32, name="acc_%d" % first) for first, count in groups]
         out_sb = keep.tile([P, N], F32)
-        pos = [work.tile([P, N_TILE * PACK], BF16, name="pos", tag="pos") for u in units]
-        neg = [work.tile([P, N_TILE * PACK], BF16, name="neg", tag="neg") for u in units]
-        wt = [
-            work.tile([P, N_TILE * PACK], BF16, name="wt", tag="wt", align_bytes=64) for u in units
+
+        mask = [keep.tile([P, SLABS, count], BF16, name="mask_%d" % first) for first, count in SIGNED_GROUPS]
+        wt = [keep.tile([P, SLABS, count], BF16, name="wt_%d" % first) for first, count in SIGNED_GROUPS]
+        grouped = [
+            keep.tile([P, PASSES, count, PACK], BF16, name="grouped_%d" % first, align_bytes=64)
+            for first, count in SIGNED_GROUPS
+        ]
+        early_pos = keep.tile([P, len(EARLY), PASSES, EARLY_WIDTH, PACK], BF16)
+        early_neg = keep.tile([P, len(EARLY), PASSES, EARLY_WIDTH, PACK], BF16)
+        early_wt = keep.tile([P, len(EARLY), PASSES, EARLY_WIDTH, PACK], BF16, align_bytes=64)
+        quantize_from = [grouped[j][:] for j in range(len(SIGNED_GROUPS))] + [
+            early_wt[:, h] for h in range(len(EARLY))
         ]
 
-        def compare(u):
-            flat = w_grouped[u][:].rearrange("p n t -> p (n t)")
+        def flat(tile):
+            return tile[:].rearrange("p h g n t -> p (h g n t)")
+
+        def compare(j):
+            first, count = SIGNED_GROUPS[j]
             nc.vector.tensor_scalar(
-                out=pos[u][:], in0=flat, scalar1=thr, scalar2=alpha, op0=ALU.is_ge, op1=ALU.mult
-            )
-            nc.vector.tensor_scalar(
-                out=neg[u][:],
-                in0=flat,
-                scalar1=neg_thr,
-                scalar2=alpha,
-                op0=ALU.is_le,
-                op1=ALU.mult,
+                out=mask[j][:], in0=w_abs[:, :, first : first + count], scalar1=thr, scalar2=alpha,
+                op0=ALU.is_ge, op1=ALU.mult,
             )
 
-        def add_bias_and_store(j):
-            for first, count in COLUMN_GROUPS[j]:
-                cols = slice(first, first + count)
-                nc.vector.tensor_tensor(
-                    out=out_sb[:, cols], in0=acc[first][:], in1=bias_all[:, cols], op=ALU.add
-                )
-                nc.sync.dma_start(out=out[:, cols], in_=out_sb[:, cols])
+        def apply_sign(j):
+            first, count = SIGNED_GROUPS[j]
+            nc.vector.tensor_tensor(
+                out=wt[j][:], in0=mask[j][:], in1=w_sign[:, :, first : first + count], op=ALU.mult
+            )
+            for g in range(PASSES):
+                regroup(grouped[j][:, g], wt[j][:, g * PACK : (g + 1) * PACK, :])
 
-        compare(0)
-        for u in range(len(units)):
-            g, j = units[u]
-            nc.vector.tensor_tensor(out=wt[u][:], in0=pos[u][:], in1=neg[u][:], op=ALU.subtract)
-            if u + 1 < len(units):
-                compare(u + 1)
-            if u == 0:
-                nc.vector.quantize_mx(
-                    out=x_codes[:].rearrange("p g m -> p (g m)").bitcast(FP8X4),
-                    scales=x_scales[:].rearrange("p g m -> p (g m)"),
-                    in_=x_grouped[:].rearrange("p g m t -> p (g m t)"),
-                )
-            if g == PASSES - 1 and j > 0:
-                add_bias_and_store(j - 1)
-            for first, count in COLUMN_GROUPS[j]:
-                cols = slice(first, first + count)
-                in_unit = slice((first - j * N_TILE) * PACK, (first - j * N_TILE + count) * PACK)
-                nc.vector.quantize_mx(
-                    out=w_codes[:, g, cols].bitcast(FP8X4),
-                    scales=w_scales[:, g, cols],
-                    in_=wt[u][:, in_unit],
-                )
-            for first, count in COLUMN_GROUPS[j]:
-                cols = slice(first, first + count)
+        def quantize(j):
+            first, count = groups[j]
+            nc.vector.quantize_mx(
+                out=codes[j][:].rearrange("p g n -> p (g n)").bitcast(FP8X4),
+                scales=scales[j][:].rearrange("p g n -> p (g n)"),
+                in_=quantize_from[j].rearrange("p g n t -> p (g n t)"),
+            )
+            for g in range(PASSES):
                 nc.tensor.matmul_mx(
-                    out=acc[first][:],
+                    out=acc[j][:],
                     lhsT=x_codes[:, g, :].bitcast(FP8X4),
                     lhsT_scale=x_scales[:, g, :],
-                    rhs=w_codes[:, g, cols].bitcast(FP8X4),
-                    rhs_scale=w_scales[:, g, cols],
+                    rhs=codes[j][:, g, :].bitcast(FP8X4),
+                    rhs_scale=scales[j][:, g, :],
                     start=(g == 0),
                     stop=(g == PASSES - 1),
                 )
-        add_bias_and_store(N_TILES - 1)
+
+        def add_bias_and_store(j):
+            first, count = groups[j]
+            cols = slice(first, first + count)
+            nc.vector.tensor_tensor(out=out_sb[:, cols], in0=acc[j][:], in1=bias_all[:, cols], op=ALU.add)
+            nc.sync.dma_start(out=out[:, cols], in_=out_sb[:, cols])
+
+        compare(0)
+        apply_sign(0)
+        compare(1)
+        apply_sign(1)
+        compare(2)
+        nc.vector.quantize_mx(
+            out=x_codes[:].rearrange("p g m -> p (g m)").bitcast(FP8X4),
+            scales=x_scales[:].rearrange("p g m -> p (g m)"),
+            in_=x_grouped[:].rearrange("p g m t -> p (g m t)"),
+        )
+        apply_sign(2)
+        compare(3)
+        quantize(0)
+        apply_sign(3)
+        nc.vector.tensor_scalar(
+            out=flat(early_pos), in0=flat(early), scalar1=thr, scalar2=alpha, op0=ALU.is_ge, op1=ALU.mult
+        )
+        nc.vector.tensor_scalar(
+            out=flat(early_neg), in0=flat(early), scalar1=neg_thr, scalar2=alpha, op0=ALU.is_le, op1=ALU.mult
+        )
+        quantize(1)
+        nc.vector.tensor_tensor(out=flat(early_wt), in0=flat(early_pos), in1=flat(early_neg), op=ALU.subtract)
+        add_bias_and_store(0)
+        quantize(2)
+        add_bias_and_store(1)
+        quantize(3)
+        quantize(4)
+        add_bias_and_store(2)
+        quantize(5)
+        add_bias_and_store(3)
+        add_bias_and_store(4)
+        add_bias_and_store(5)

@@ -17,6 +17,7 @@ PACK = 4
 M, K, N = 128, 1024, 1024
 PASSES = K // (P * PACK)
 SLABS = K // P
+PAIRS = SLABS // 2
 SIGNED_GROUPS = [(0, 128), (128, 256), (384, 256), (640, 128)]
 SIGNED = 768
 EARLY = [(768, 128), (896, 128)]
@@ -25,7 +26,6 @@ THRESHOLD_FACTOR = 0.7
 MAGNITUDE_BITS = 0x7FFF7FFF
 SIGN_BITS = 0x80008000 - (1 << 32)
 ONES_BITS = 0x3F803F80
-SCALAR_SIGN_SLABS = (0, 1, 4)
 
 FLOPS = 2 * M * K * N
 
@@ -41,7 +41,7 @@ def tile_ternarydense_s_kernel(tc, x, w, b, out):
         nc.vector.memset(ones[:], 1.0)
         one_col = keep.tile([P, 1], BF16)
         nc.vector.memset(one_col[:], 1.0)
-        ident = keep.tile([P, P], BF16)
+        ident = keep.tile([P, P], F32)
         make_identity(nc, ident[:])
         mean = 1.0 / (K * N)
         factors = keep.tile([P, 3], F32)
@@ -49,8 +49,11 @@ def tile_ternarydense_s_kernel(tc, x, w, b, out):
             nc.vector.memset(factors[:, i : i + 1], factor)
 
         w_sb = keep.tile([P, SLABS, N], BF16)
-        for r in range(SLABS):
-            nc.sync.dma_start(out=w_sb[:, r, :], in_=w[r * P : (r + 1) * P, :])
+        w_rows = w.rearrange("(s p e) n -> s p e n", p=P, e=2)
+        for s in range(PAIRS - 1):
+            nc.sync.dma_start(out=w_sb[:, 2 * s : 2 * s + 2, :], in_=w_rows[s])
+        for e in range(2):
+            nc.sync.dma_start(out=w_sb[:, SLABS - 2 + e, :], in_=w_rows[PAIRS - 1, :, e, :])
         x_sb = keep.tile([P, K], BF16)
         nc.sync.dma_start(out=x_sb[:], in_=x)
         bias_all = keep.tile([P, N], BF16)
@@ -63,35 +66,40 @@ def tile_ternarydense_s_kernel(tc, x, w, b, out):
         total = sums[:, 1:2]
         early = keep.tile([P, len(EARLY), PASSES, EARLY_WIDTH, PACK], BF16)
 
-        def magnitude(r):
+        def magnitude(first, count):
             nc.vector.tensor_scalar(
-                out=w_abs[:, r, :].bitcast(I32),
-                in0=w_sb[:, r, :].bitcast(I32),
+                out=w_abs[:, first : first + count, :].bitcast(I32),
+                in0=w_sb[:, first : first + count, :].bitcast(I32),
                 scalar1=MAGNITUDE_BITS,
                 scalar2=None,
                 op0=ALU.bitwise_and,
             )
-            for c in range(N // P):
-                nc.tensor.matmul(
-                    out=partial,
-                    lhsT=w_abs[:, r, c * P : (c + 1) * P],
-                    rhs=one_col[:],
-                    start=(r == 0 and c == 0),
-                    stop=(r == SLABS - 1 and c == N // P - 1),
-                )
+            for r in range(first, first + count):
+                for c in range(N // P):
+                    nc.tensor.matmul(
+                        out=partial,
+                        lhsT=w_abs[:, r, c * P : (c + 1) * P],
+                        rhs=one_col[:],
+                        start=(r == 0 and c == 0),
+                        stop=(r == SLABS - 1 and c == N // P - 1),
+                    )
 
-        def vector_sign(r):
+        def vector_sign(first, count):
             nc.vector.tensor_scalar(
-                out=w_sign[:, r, :].bitcast(I32),
-                in0=w_sb[:, r, 0:SIGNED].bitcast(I32),
+                out=w_sign[:, first : first + count, :].bitcast(I32),
+                in0=w_sb[:, first : first + count, 0:SIGNED].bitcast(I32),
                 scalar1=SIGN_BITS,
                 scalar2=ONES_BITS,
                 op0=ALU.bitwise_and,
                 op1=ALU.bitwise_or,
             )
 
-        def scalar_sign(r):
-            nc.scalar.activation(out=w_sign[:, r, :], in_=w_sb[:, r, 0:SIGNED], func=ACT.Sign)
+        def scalar_sign(first, count):
+            nc.scalar.activation(
+                out=w_sign[:, first : first + count, :],
+                in_=w_sb[:, first : first + count, 0:SIGNED],
+                func=ACT.Sign,
+            )
 
         def regroup(dst, src):
             nc.scalar.copy(
@@ -103,14 +111,18 @@ def tile_ternarydense_s_kernel(tc, x, w, b, out):
             for h, (first, count) in enumerate(EARLY):
                 regroup(early[:, h, g], w_sb[:, g * PACK : (g + 1) * PACK, first : first + count])
 
-        for r in range(SLABS):
-            magnitude(r)
-            if r in SCALAR_SIGN_SLABS:
-                scalar_sign(r)
-            else:
-                vector_sign(r)
-            if r == PACK - 1:
-                regroup_early(0)
+        magnitude(0, 2)
+        scalar_sign(0, 2)
+        magnitude(2, 2)
+        vector_sign(2, 2)
+        regroup_early(0)
+        magnitude(4, 2)
+        scalar_sign(4, 1)
+        vector_sign(5, 1)
+        magnitude(6, 1)
+        vector_sign(6, 1)
+        magnitude(7, 1)
+        vector_sign(7, 1)
         regroup_early(1)
         partial_sb = keep.tile([P, 1], F32)
         nc.vector.tensor_copy(out=partial_sb[:], in_=partial)
@@ -124,11 +136,14 @@ def tile_ternarydense_s_kernel(tc, x, w, b, out):
         thr = levels[:, 1:2]
         neg_thr = levels[:, 2:3]
 
-        x_t = psum.tile([P, SLABS, M], BF16)
-        for r in range(SLABS):
-            nc.tensor.transpose(x_t[:, r, :], x_sb[:, r * P : (r + 1) * P], ident[:])
+        x_words = x_sb[:].bitcast(F32)
+        x_t = psum.tile([P, PAIRS, M], F32)
+        for s in range(PAIRS):
+            nc.tensor.transpose(x_t[:, s, :], x_words[:, s * P : (s + 1) * P], ident[:])
         x_grouped = keep.tile([P, PASSES, M, PACK], BF16, align_bytes=64)
-        nc.scalar.copy(out=x_grouped[:], in_=x_t[:].rearrange("p (g t) m -> p g m t", t=PACK))
+        nc.scalar.copy(
+            out=x_grouped[:].bitcast(F32), in_=x_t[:].rearrange("p (g u) m -> p g m u", g=PASSES)
+        )
         x_codes = keep.tile([P, PASSES, M], U32, align_bytes=64)
         x_scales = keep.tile([P, PASSES, M], U8, align_bytes=64)
 

@@ -11,6 +11,7 @@ U8 = mybir.dt.uint8
 FP8X4 = mybir.dt.float8_e4m3fn_x4
 ALU = mybir.AluOpType
 ACT = mybir.ActivationFunctionType
+AXIS_X = mybir.AxisListType.X
 
 P = 128
 PACK = 4
@@ -18,14 +19,10 @@ M, K, N = 128, 1024, 1024
 PASSES = K // (P * PACK)
 SLABS = K // P
 PAIRS = SLABS // 2
-SIGNED_GROUPS = [(0, 128), (128, 256), (384, 256), (640, 128)]
-SIGNED = 768
-EARLY = [(768, 128), (896, 128)]
-EARLY_WIDTH = 128
+SPLIT = 512
 THRESHOLD_FACTOR = 0.7
 MAGNITUDE_BITS = 0x7FFF7FFF
 SIGN_BITS = 0x80008000 - (1 << 32)
-ONES_BITS = 0x3F803F80
 
 FLOPS = 2 * M * K * N
 
@@ -45,96 +42,106 @@ def tile_ternarydense_s_kernel(tc, x, w, b, out):
         make_identity(nc, ident[:])
         mean = 1.0 / (K * N)
         factors = keep.tile([P, 3], F32)
-        for i, factor in enumerate((mean, THRESHOLD_FACTOR * mean, -THRESHOLD_FACTOR * mean)):
+        for i, factor in enumerate((mean, 2 * mean, THRESHOLD_FACTOR * mean)):
             nc.vector.memset(factors[:, i : i + 1], factor)
 
         w_sb = keep.tile([P, SLABS, N], BF16)
         w_rows = w.rearrange("(s p e) n -> s p e n", p=P, e=2)
-        for s in range(PAIRS - 1):
-            nc.sync.dma_start(out=w_sb[:, 2 * s : 2 * s + 2, :], in_=w_rows[s])
-        for e in range(2):
-            nc.sync.dma_start(out=w_sb[:, SLABS - 2 + e, :], in_=w_rows[PAIRS - 1, :, e, :])
+
+        def load(first, count, lo, hi):
+            s, e = divmod(first, 2)
+            nc.sync.dma_start(
+                out=w_sb[:, first : first + count, lo:hi], in_=w_rows[s, :, e : e + count, lo:hi]
+            )
+
+        for r in range(SLABS - 1):
+            load(r, 1, 0, N)
+        load(7, 1, 0, SPLIT)
+        load(7, 1, SPLIT, N)
         x_sb = keep.tile([P, K], BF16)
         nc.sync.dma_start(out=x_sb[:], in_=x)
         bias_all = keep.tile([P, N], BF16)
         nc.sync.dma_start(out=bias_all[:], in_=b.partition_broadcast(P))
 
         w_abs = keep.tile([P, SLABS, N], BF16)
-        w_sign = keep.tile([P, SLABS, SIGNED], BF16)
+        abs_grouped = keep.tile([P, SPLIT, PACK], BF16)
+        sign_grouped = keep.tile([P, SPLIT, PACK], BF16)
+        scalar_sums = keep.tile([P, 4], F32)
+        vector_sum = keep.tile([P, 1], F32)
         sums = psum.tile([P, 2], F32)
         partial = sums[:, 0:1]
         total = sums[:, 1:2]
-        early = keep.tile([P, len(EARLY), PASSES, EARLY_WIDTH, PACK], BF16)
+        blocks = [
+            (r, c)
+            for r in range(3, SLABS)
+            for c in range(N // P)
+            if (r >= PACK or c * P >= SPLIT) and (r < 7 or c * P < SPLIT)
+        ]
 
-        def magnitude(first, count):
+        def magnitude(first, count, lo, hi):
             nc.vector.tensor_scalar(
-                out=w_abs[:, first : first + count, :].bitcast(I32),
-                in0=w_sb[:, first : first + count, :].bitcast(I32),
+                out=w_abs[:, first : first + count, lo:hi].bitcast(I32),
+                in0=w_sb[:, first : first + count, lo:hi].bitcast(I32),
                 scalar1=MAGNITUDE_BITS,
                 scalar2=None,
                 op0=ALU.bitwise_and,
             )
             for r in range(first, first + count):
-                for c in range(N // P):
+                for c in range(lo // P, hi // P):
                     nc.tensor.matmul(
                         out=partial,
                         lhsT=w_abs[:, r, c * P : (c + 1) * P],
                         rhs=one_col[:],
-                        start=(r == 0 and c == 0),
-                        stop=(r == SLABS - 1 and c == N // P - 1),
+                        start=((r, c) == blocks[0]),
+                        stop=((r, c) == blocks[-1]),
                     )
 
-        def vector_sign(first, count):
+        def by_column(tile):
+            return tile.rearrange("p (c i) t -> p c t i", i=4)
+
+        def by_slab(tile):
+            return tile.rearrange("p t (c i) -> p c t i", i=4)
+
+        def vector_sign_grouped(lo, hi):
             nc.vector.tensor_scalar(
-                out=w_sign[:, first : first + count, :].bitcast(I32),
-                in0=w_sb[:, first : first + count, 0:SIGNED].bitcast(I32),
-                scalar1=SIGN_BITS,
-                scalar2=ONES_BITS,
-                op0=ALU.bitwise_and,
-                op1=ALU.bitwise_or,
+                out=by_column(sign_grouped[:, lo:hi]), in0=by_slab(w_sb[:, 0:PACK, lo:hi]),
+                scalar1=0.0, scalar2=0.5, op0=ALU.is_ge, op1=ALU.subtract,
             )
 
-        def scalar_sign(first, count):
+        for r in range(3):
             nc.scalar.activation(
-                out=w_sign[:, first : first + count, :],
-                in_=w_sb[:, first : first + count, 0:SIGNED],
-                func=ACT.Sign,
+                out=w_abs[:, r, SPLIT:N], in_=w_sb[:, r, SPLIT:N], func=ACT.Abs,
+                accum_out=scalar_sums[:, r : r + 1],
             )
-
-        def regroup(dst, src):
-            nc.scalar.copy(
-                out=dst.rearrange("p (c i) t -> p c t i", i=4),
-                in_=src.rearrange("p t (c i) -> p c t i", i=4),
-            )
-
-        def regroup_early(g):
-            for h, (first, count) in enumerate(EARLY):
-                regroup(early[:, h, g], w_sb[:, g * PACK : (g + 1) * PACK, first : first + count])
-
-        magnitude(0, 2)
-        scalar_sign(0, 2)
-        magnitude(2, 2)
-        vector_sign(2, 2)
-        regroup_early(0)
-        magnitude(4, 2)
-        scalar_sign(4, 1)
-        vector_sign(5, 1)
-        magnitude(6, 1)
-        vector_sign(6, 1)
-        magnitude(7, 1)
-        vector_sign(7, 1)
-        regroup_early(1)
-        partial_sb = keep.tile([P, 1], F32)
-        nc.vector.tensor_copy(out=partial_sb[:], in_=partial)
-        nc.tensor.matmul(out=total, lhsT=ones[:], rhs=partial_sb[:], start=True, stop=True)
-
+        nc.scalar.activation(
+            out=by_column(abs_grouped[:]), in_=by_slab(w_sb[:, 0:PACK, 0:SPLIT]), func=ACT.Abs,
+            accum_out=scalar_sums[:, 3:4],
+        )
+        magnitude(3, 1, SPLIT, N)
+        vector_sign_grouped(0, SPLIT // 2)
+        magnitude(4, 1, 0, N)
+        magnitude(5, 1, 0, N)
+        vector_sign_grouped(SPLIT // 2, SPLIT)
+        magnitude(6, 1, 0, N)
+        magnitude(7, 1, 0, SPLIT)
+        nc.vector.scalar_tensor_tensor(
+            out=w_abs[:, 7, SPLIT:N], in0=w_sb[:, 7, SPLIT:N], scalar=-1.0, in1=w_sb[:, 7, SPLIT:N],
+            op0=ALU.mult, op1=ALU.max, accum_out=vector_sum[:],
+        )
+        scalar_sum = keep.tile([P, 1], F32)
+        nc.vector.tensor_reduce(out=scalar_sum[:], in_=scalar_sums[:], axis=AXIS_X, op=ALU.add)
+        other_sums = keep.tile([P, 1], F32)
+        nc.vector.tensor_tensor(out=other_sums[:], in0=scalar_sum[:], in1=vector_sum[:], op=ALU.add)
+        row_sum = keep.tile([P, 1], F32)
+        nc.vector.tensor_tensor(out=row_sum[:], in0=partial, in1=other_sums[:], op=ALU.add)
+        nc.tensor.matmul(out=total, lhsT=ones[:], rhs=row_sum[:], start=True, stop=True)
         levels = keep.tile([P, 3], F32)
         nc.vector.tensor_tensor(
             out=levels[:], in0=total.to_broadcast([P, 3]), in1=factors[:], op=ALU.mult
         )
         alpha = levels[:, 0:1]
-        thr = levels[:, 1:2]
-        neg_thr = levels[:, 2:3]
+        twice_alpha = levels[:, 1:2]
+        thr = levels[:, 2:3]
 
         x_words = x_sb[:].bitcast(F32)
         x_t = psum.tile([P, PAIRS, M], F32)
@@ -147,102 +154,115 @@ def tile_ternarydense_s_kernel(tc, x, w, b, out):
         x_codes = keep.tile([P, PASSES, M], U32, align_bytes=64)
         x_scales = keep.tile([P, PASSES, M], U8, align_bytes=64)
 
-        groups = SIGNED_GROUPS + EARLY
-        codes = [
-            keep.tile([P, PASSES, count], U32, name="codes_%d" % first, align_bytes=64)
-            for first, count in groups
+        w_codes = {}
+        w_scales = {}
+        acc_first = (0, 512, 768)
+        acc_count = (512, 256, 256)
+        acc = [
+            psum.tile([P, count], F32, name="acc_%d" % first)
+            for first, count in zip(acc_first, acc_count)
         ]
-        scales = [
-            keep.tile([P, PASSES, count], U8, name="scales_%d" % first, align_bytes=64)
-            for first, count in groups
-        ]
-        acc = [psum.tile([P, count], F32, name="acc_%d" % first) for first, count in groups]
+        passes_done = [0] * len(acc)
         out_sb = keep.tile([P, N], F32)
+        tiles = {}
 
-        mask = [keep.tile([P, SLABS, count], BF16, name="mask_%d" % first) for first, count in SIGNED_GROUPS]
-        wt = [keep.tile([P, SLABS, count], BF16, name="wt_%d" % first) for first, count in SIGNED_GROUPS]
-        grouped = [
-            keep.tile([P, PASSES, count, PACK], BF16, name="grouped_%d" % first, align_bytes=64)
-            for first, count in SIGNED_GROUPS
-        ]
-        early_pos = keep.tile([P, len(EARLY), PASSES, EARLY_WIDTH, PACK], BF16)
-        early_neg = keep.tile([P, len(EARLY), PASSES, EARLY_WIDTH, PACK], BF16)
-        early_wt = keep.tile([P, len(EARLY), PASSES, EARLY_WIDTH, PACK], BF16, align_bytes=64)
-        quantize_from = [grouped[j][:] for j in range(len(SIGNED_GROUPS))] + [
-            early_wt[:, h] for h in range(len(EARLY))
-        ]
+        def new_tile(what, unit, shape):
+            tiles[what, unit] = keep.tile(
+                shape, BF16, name="%s_%d_%d_%d_%d" % ((what,) + unit), align_bytes=64
+            )
+            return tiles[what, unit]
 
-        def flat(tile):
-            return tile[:].rearrange("p h g n t -> p (h g n t)")
-
-        def compare(j):
-            first, count = SIGNED_GROUPS[j]
+        def compare(unit):
+            g, gs, first, count = unit
+            mask = new_tile("mask", unit, [P, gs * PACK, count])
             nc.vector.tensor_scalar(
-                out=mask[j][:], in0=w_abs[:, :, first : first + count], scalar1=thr, scalar2=alpha,
-                op0=ALU.is_ge, op1=ALU.mult,
+                out=mask[:],
+                in0=w_abs[:, g * PACK : (g + gs) * PACK, first : first + count],
+                scalar1=thr,
+                scalar2=None,
+                op0=ALU.is_ge,
             )
 
-        def apply_sign(j):
-            first, count = SIGNED_GROUPS[j]
-            nc.vector.tensor_tensor(
-                out=wt[j][:], in0=mask[j][:], in1=w_sign[:, :, first : first + count], op=ALU.mult
+        def apply_sign(unit, lo, hi):
+            g, gs, first, count = unit
+            if ("ternary", unit) not in tiles:
+                new_tile("ternary", unit, [P, gs * PACK, count])
+                new_tile("grouped", unit, [P, gs, count, PACK])
+            ternary = tiles["ternary", unit]
+            nc.vector.scalar_tensor_tensor(
+                out=ternary[:, :, lo:hi].bitcast(I32),
+                in0=w_sb[:, g * PACK : (g + gs) * PACK, first + lo : first + hi].bitcast(I32),
+                scalar=SIGN_BITS,
+                in1=tiles["mask", unit][:, :, lo:hi].bitcast(I32),
+                op0=ALU.bitwise_and,
+                op1=ALU.bitwise_or,
             )
-            for g in range(PASSES):
-                regroup(grouped[j][:, g], wt[j][:, g * PACK : (g + 1) * PACK, :])
-
-        def quantize(j):
-            first, count = groups[j]
-            nc.vector.quantize_mx(
-                out=codes[j][:].rearrange("p g n -> p (g n)").bitcast(FP8X4),
-                scales=scales[j][:].rearrange("p g n -> p (g n)"),
-                in_=quantize_from[j].rearrange("p g n t -> p (g n t)"),
-            )
-            for g in range(PASSES):
-                nc.tensor.matmul_mx(
-                    out=acc[j][:],
-                    lhsT=x_codes[:, g, :].bitcast(FP8X4),
-                    lhsT_scale=x_scales[:, g, :],
-                    rhs=codes[j][:, g, :].bitcast(FP8X4),
-                    rhs_scale=scales[j][:, g, :],
-                    start=(g == 0),
-                    stop=(g == PASSES - 1),
+            for i in range(gs):
+                nc.scalar.activation(
+                    out=by_column(tiles["grouped", unit][:, i, lo:hi]),
+                    in_=by_slab(ternary[:, i * PACK : (i + 1) * PACK, lo:hi]),
+                    func=ACT.Copy,
+                    scale=alpha,
                 )
 
+        def quantize(unit):
+            g, gs, first, count = unit
+            codes = keep.tile([P, gs, count], U32, name="codes_%d_%d" % (g, first), align_bytes=64)
+            scales = keep.tile([P, gs, count], U8, name="scales_%d_%d" % (g, first), align_bytes=64)
+            nc.vector.quantize_mx(
+                out=codes[:].rearrange("p g n -> p (g n)").bitcast(FP8X4),
+                scales=scales[:].rearrange("p g n -> p (g n)"),
+                in_=tiles["grouped", unit][:].rearrange("p g n t -> p (g n t)"),
+            )
+            j = acc_first.index(first)
+            for i in range(gs):
+                nc.tensor.matmul_mx(
+                    out=acc[j][:],
+                    lhsT=x_codes[:, g + i, :].bitcast(FP8X4),
+                    lhsT_scale=x_scales[:, g + i, :],
+                    rhs=codes[:, i, :].bitcast(FP8X4),
+                    rhs_scale=scales[:, i, :],
+                    start=(passes_done[j] == 0),
+                    stop=(passes_done[j] == PASSES - 1),
+                )
+                passes_done[j] += 1
+
         def add_bias_and_store(j):
-            first, count = groups[j]
-            cols = slice(first, first + count)
+            cols = slice(acc_first[j], acc_first[j] + acc_count[j])
             nc.vector.tensor_tensor(out=out_sb[:, cols], in0=acc[j][:], in1=bias_all[:, cols], op=ALU.add)
             nc.sync.dma_start(out=out[:, cols], in_=out_sb[:, cols])
 
-        compare(0)
-        apply_sign(0)
-        compare(1)
-        apply_sign(1)
-        compare(2)
+        early = (0, 1, 0, SPLIT)
+        a = (1, 1, 0, SPLIT)
+        b0 = (0, 2, 512, 256)
+        b1 = (0, 2, 768, 256)
+
+        compare(a)
+        compare(b0)
+        apply_sign(a, 0, 256)
+        apply_sign(a, 256, 512)
+        apply_sign(b0, 0, 256)
+        compare(b1)
+        apply_sign(b1, 0, 256)
+        early_mask = keep.tile([P, SPLIT * PACK], BF16)
+        nc.vector.tensor_scalar(
+            out=early_mask[:], in0=abs_grouped[:].rearrange("p n t -> p (n t)"),
+            scalar1=thr, scalar2=twice_alpha, op0=ALU.is_ge, op1=ALU.mult,
+        )
         nc.vector.quantize_mx(
             out=x_codes[:].rearrange("p g m -> p (g m)").bitcast(FP8X4),
             scales=x_scales[:].rearrange("p g m -> p (g m)"),
             in_=x_grouped[:].rearrange("p g m t -> p (g m t)"),
         )
-        apply_sign(2)
-        compare(3)
-        quantize(0)
-        apply_sign(3)
-        nc.vector.tensor_scalar(
-            out=flat(early_pos), in0=flat(early), scalar1=thr, scalar2=alpha, op0=ALU.is_ge, op1=ALU.mult
+        early_wt = new_tile("grouped", early, [P, 1, SPLIT, PACK])
+        nc.vector.tensor_tensor(
+            out=early_wt[:].rearrange("p g n t -> p (g n t)"), in0=early_mask[:],
+            in1=sign_grouped[:].rearrange("p n t -> p (n t)"), op=ALU.mult,
         )
-        nc.vector.tensor_scalar(
-            out=flat(early_neg), in0=flat(early), scalar1=neg_thr, scalar2=alpha, op0=ALU.is_le, op1=ALU.mult
-        )
-        quantize(1)
-        nc.vector.tensor_tensor(out=flat(early_wt), in0=flat(early_pos), in1=flat(early_neg), op=ALU.subtract)
+        quantize(a)
+        quantize(early)
+        quantize(b0)
+        quantize(b1)
         add_bias_and_store(0)
-        quantize(2)
         add_bias_and_store(1)
-        quantize(3)
-        quantize(4)
         add_bias_and_store(2)
-        quantize(5)
-        add_bias_and_store(3)
-        add_bias_and_store(4)
-        add_bias_and_store(5)

@@ -19,10 +19,14 @@ M, K, N = 128, 1024, 1024
 PASSES = K // (P * PACK)
 SLABS = K // P
 PAIRS = SLABS // 2
-SPLIT = 512
 THRESHOLD_FACTOR = 0.7
+MEAN = 1.0 / (K * N)
+KEEP_FROM = 2.0 - 2.0**-8
 MAGNITUDE_BITS = 0x7FFF7FFF
-SIGN_BITS = 0x80008000 - (1 << 32)
+KEEP_BITS = 0xC000C000 - (1 << 32)
+SPLIT = 640
+LAST_SPLIT = 640
+EARLY = 768
 
 FLOPS = 2 * M * K * N
 
@@ -40,61 +44,24 @@ def tile_ternarydense_s_kernel(tc, x, w, b, out):
         nc.vector.memset(one_col[:], 1.0)
         ident = keep.tile([P, P], F32)
         make_identity(nc, ident[:])
-        mean = 1.0 / (K * N)
-        factors = keep.tile([P, 3], F32)
-        for i, factor in enumerate((mean, 2 * mean, THRESHOLD_FACTOR * mean)):
-            nc.vector.memset(factors[:, i : i + 1], factor)
 
         w_sb = keep.tile([P, SLABS, N], BF16)
-        w_rows = w.rearrange("(s p e) n -> s p e n", p=P, e=2)
-
-        def load(first, count, lo, hi):
-            s, e = divmod(first, 2)
-            nc.sync.dma_start(
-                out=w_sb[:, first : first + count, lo:hi], in_=w_rows[s, :, e : e + count, lo:hi]
-            )
-
+        w_rows = w.rearrange("(s p e) n -> s e p n", p=P, e=2)
         for r in range(SLABS - 1):
-            load(r, 1, 0, N)
-        load(7, 1, 0, SPLIT)
-        load(7, 1, SPLIT, N)
+            nc.sync.dma_start(out=w_sb[:, r, :], in_=w_rows[r // 2, r % 2])
+        last = SLABS - 1
+        for lo, hi in ((0, LAST_SPLIT), (LAST_SPLIT, N)):
+            nc.sync.dma_start(out=w_sb[:, last, lo:hi], in_=w_rows[last // 2, last % 2, :, lo:hi])
         x_sb = keep.tile([P, K], BF16)
         nc.sync.dma_start(out=x_sb[:], in_=x)
         bias_all = keep.tile([P, N], BF16)
         nc.sync.dma_start(out=bias_all[:], in_=b.partition_broadcast(P))
 
-        w_abs = keep.tile([P, SLABS, N], BF16)
-        abs_grouped = keep.tile([P, SPLIT, PACK], BF16)
-        sign_grouped = keep.tile([P, SPLIT, PACK], BF16)
-        scalar_sums = keep.tile([P, 4], F32)
-        vector_sum = keep.tile([P, 1], F32)
-        sums = psum.tile([P, 2], F32)
-        partial = sums[:, 0:1]
-        total = sums[:, 1:2]
-        blocks = [
-            (r, c)
-            for r in range(3, SLABS)
-            for c in range(N // P)
-            if (r >= PACK or c * P >= SPLIT) and (r < 7 or c * P < SPLIT)
-        ]
-
-        def magnitude(first, count, lo, hi):
-            nc.vector.tensor_scalar(
-                out=w_abs[:, first : first + count, lo:hi].bitcast(I32),
-                in0=w_sb[:, first : first + count, lo:hi].bitcast(I32),
-                scalar1=MAGNITUDE_BITS,
-                scalar2=None,
-                op0=ALU.bitwise_and,
-            )
-            for r in range(first, first + count):
-                for c in range(lo // P, hi // P):
-                    nc.tensor.matmul(
-                        out=partial,
-                        lhsT=w_abs[:, r, c * P : (c + 1) * P],
-                        rhs=one_col[:],
-                        start=((r, c) == blocks[0]),
-                        stop=((r, c) == blocks[-1]),
-                    )
+        scalar_sums = keep.tile([P, SLABS + 8], F32)
+        w_abs = keep.tile([P, SLABS - 1, SPLIT], BF16)
+        scratch = keep.tile([P, SLABS, N], BF16)
+        partial = psum.tile([P, 1], F32)
+        total = psum.tile([P, 1], F32)
 
         def by_column(tile):
             return tile.rearrange("p (c i) t -> p c t i", i=4)
@@ -102,167 +69,170 @@ def tile_ternarydense_s_kernel(tc, x, w, b, out):
         def by_slab(tile):
             return tile.rearrange("p t (c i) -> p c t i", i=4)
 
-        def vector_sign_grouped(lo, hi):
-            nc.vector.tensor_scalar(
-                out=by_column(sign_grouped[:, lo:hi]), in0=by_slab(w_sb[:, 0:PACK, lo:hi]),
-                scalar1=0.0, scalar2=0.5, op0=ALU.is_ge, op1=ALU.subtract,
-            )
-
-        for r in range(3):
+        early_w = keep.tile([P, N - EARLY, PACK], BF16)
+        blocks = [(r, c) for r in range(last) for c in range(SPLIT // P)]
+        for r in range(SLABS):
+            split = SPLIT if r < last else LAST_SPLIT
             nc.scalar.activation(
-                out=w_abs[:, r, SPLIT:N], in_=w_sb[:, r, SPLIT:N], func=ACT.Abs,
+                out=scratch[:, r, split:N], in_=w_sb[:, r, split:N], func=ACT.Abs,
                 accum_out=scalar_sums[:, r : r + 1],
             )
-        nc.scalar.activation(
-            out=by_column(abs_grouped[:]), in_=by_slab(w_sb[:, 0:PACK, 0:SPLIT]), func=ACT.Abs,
-            accum_out=scalar_sums[:, 3:4],
-        )
-        magnitude(3, 1, SPLIT, N)
-        vector_sign_grouped(0, SPLIT // 2)
-        magnitude(4, 1, 0, N)
-        magnitude(5, 1, 0, N)
-        vector_sign_grouped(SPLIT // 2, SPLIT)
-        magnitude(6, 1, 0, N)
-        magnitude(7, 1, 0, SPLIT)
-        nc.vector.scalar_tensor_tensor(
-            out=w_abs[:, 7, SPLIT:N], in0=w_sb[:, 7, SPLIT:N], scalar=-1.0, in1=w_sb[:, 7, SPLIT:N],
-            op0=ALU.mult, op1=ALU.max, accum_out=vector_sum[:],
-        )
-        scalar_sum = keep.tile([P, 1], F32)
-        nc.vector.tensor_reduce(out=scalar_sum[:], in_=scalar_sums[:], axis=AXIS_X, op=ALU.add)
-        other_sums = keep.tile([P, 1], F32)
-        nc.vector.tensor_tensor(out=other_sums[:], in0=scalar_sum[:], in1=vector_sum[:], op=ALU.add)
+            if r == last:
+                nc.vector.scalar_tensor_tensor(
+                    out=scratch[:, r, 0:split], in0=w_sb[:, r, 0:split], scalar=-1.0,
+                    in1=w_sb[:, r, 0:split], op0=ALU.mult, op1=ALU.max,
+                    accum_out=scalar_sums[:, SLABS + 1 : SLABS + 2],
+                )
+                continue
+            nc.vector.tensor_scalar(
+                out=w_abs[:, r, :].bitcast(I32), in0=w_sb[:, r, 0:SPLIT].bitcast(I32),
+                scalar1=MAGNITUDE_BITS, scalar2=None, op0=ALU.bitwise_and,
+            )
+            for c in range(SPLIT // P):
+                nc.tensor.matmul(
+                    out=partial[:], lhsT=w_abs[:, r, c * P : (c + 1) * P], rhs=one_col[:],
+                    start=((r, c) == blocks[0]), stop=((r, c) == blocks[-1]),
+                )
+            if r == PACK - 1:
+                nc.vector.tensor_copy(
+                    out=by_column(early_w[:]), in_=by_slab(w_sb[:, 0:PACK, EARLY:N])
+                )
+        nc.vector.tensor_copy(out=scalar_sums[:, SLABS : SLABS + 1], in_=partial[:])
         row_sum = keep.tile([P, 1], F32)
-        nc.vector.tensor_tensor(out=row_sum[:], in0=partial, in1=other_sums[:], op=ALU.add)
-        nc.tensor.matmul(out=total, lhsT=ones[:], rhs=row_sum[:], start=True, stop=True)
-        levels = keep.tile([P, 3], F32)
-        nc.vector.tensor_tensor(
-            out=levels[:], in0=total.to_broadcast([P, 3]), in1=factors[:], op=ALU.mult
+        nc.vector.tensor_reduce(
+            out=row_sum[:], in_=scalar_sums[:, 0 : SLABS + 2], axis=AXIS_X, op=ALU.add
         )
-        alpha = levels[:, 0:1]
-        twice_alpha = levels[:, 1:2]
-        thr = levels[:, 2:3]
+        nc.tensor.matmul(out=total[:], lhsT=ones[:], rhs=row_sum[:], start=True, stop=True)
+        inverse = keep.tile([P, 1], F32)
+        nc.vector.reciprocal(out=inverse[:], in_=total[:])
+        to_two = keep.tile([P, 1], F32)
+        nc.vector.tensor_scalar(
+            out=to_two[:], in0=inverse[:], scalar1=KEEP_FROM / (THRESHOLD_FACTOR * MEAN), scalar2=None,
+            op0=ALU.mult,
+        )
+        half_alpha = keep.tile([P, 1], F32)
+        nc.vector.tensor_scalar(
+            out=half_alpha[:], in0=total[:], scalar1=MEAN / 2, scalar2=None, op0=ALU.mult
+        )
 
         x_words = x_sb[:].bitcast(F32)
         x_t = psum.tile([P, PAIRS, M], F32)
         for s in range(PAIRS):
             nc.tensor.transpose(x_t[:, s, :], x_words[:, s * P : (s + 1) * P], ident[:])
         x_grouped = keep.tile([P, PASSES, M, PACK], BF16, align_bytes=64)
-        nc.scalar.copy(
-            out=x_grouped[:].bitcast(F32), in_=x_t[:].rearrange("p (g u) m -> p g m u", g=PASSES)
-        )
         x_codes = keep.tile([P, PASSES, M], U32, align_bytes=64)
         x_scales = keep.tile([P, PASSES, M], U8, align_bytes=64)
 
-        w_codes = {}
-        w_scales = {}
-        acc_first = (0, 512, 768)
-        acc_count = (512, 256, 256)
-        acc = [
-            psum.tile([P, count], F32, name="acc_%d" % first)
-            for first, count in zip(acc_first, acc_count)
-        ]
+        acc_first = (0, 256, 512, 768)
+        acc = [psum.tile([P, 256], F32, name="acc_%d" % first) for first in acc_first]
         passes_done = [0] * len(acc)
         out_sb = keep.tile([P, N], F32)
-        tiles = {}
+        scaled = [keep.tile([P, SLABS, 256], BF16, name="scaled_%d" % first) for first in acc_first]
+        signs = [keep.tile([P, SLABS, 256], BF16, name="signs_%d" % first) for first in acc_first]
+        grouped = keep.tile([P, N // 256, PASSES, 256, PACK], BF16, align_bytes=64)
+        early_scaled = keep.tile([P, N - EARLY, PACK], BF16)
+        early_signs = keep.tile([P, N - EARLY, PACK], BF16)
+        early_wt = keep.tile([P, N - EARLY, PACK], BF16, align_bytes=64)
+        w_codes = keep.tile([P, N // 256, PASSES, 256], U32, align_bytes=64)
+        w_scales = keep.tile([P, N // 256, PASSES, 256], U8, align_bytes=64)
 
-        def new_tile(what, unit, shape):
-            tiles[what, unit] = keep.tile(
-                shape, BF16, name="%s_%d_%d_%d_%d" % ((what,) + unit), align_bytes=64
-            )
-            return tiles[what, unit]
-
-        def compare(unit):
-            g, gs, first, count = unit
-            mask = new_tile("mask", unit, [P, gs * PACK, count])
+        def scale_to_two(dst, src):
             nc.vector.tensor_scalar(
-                out=mask[:],
-                in0=w_abs[:, g * PACK : (g + gs) * PACK, first : first + count],
-                scalar1=thr,
-                scalar2=None,
-                op0=ALU.is_ge,
+                out=dst, in0=src, scalar1=to_two[:], scalar2=None, op0=ALU.mult
             )
 
-        def apply_sign(unit, lo, hi):
-            g, gs, first, count = unit
-            if ("ternary", unit) not in tiles:
-                new_tile("ternary", unit, [P, gs * PACK, count])
-                new_tile("grouped", unit, [P, gs, count, PACK])
-            ternary = tiles["ternary", unit]
-            nc.vector.scalar_tensor_tensor(
-                out=ternary[:, :, lo:hi].bitcast(I32),
-                in0=w_sb[:, g * PACK : (g + gs) * PACK, first + lo : first + hi].bitcast(I32),
-                scalar=SIGN_BITS,
-                in1=tiles["mask", unit][:, :, lo:hi].bitcast(I32),
+        def keep_signs(dst, src):
+            nc.vector.tensor_scalar(
+                out=dst.bitcast(I32), in0=src.bitcast(I32), scalar1=KEEP_BITS, scalar2=None,
                 op0=ALU.bitwise_and,
-                op1=ALU.bitwise_or,
             )
-            for i in range(gs):
-                nc.scalar.activation(
-                    out=by_column(tiles["grouped", unit][:, i, lo:hi]),
-                    in_=by_slab(ternary[:, i * PACK : (i + 1) * PACK, lo:hi]),
-                    func=ACT.Copy,
-                    scale=alpha,
-                )
 
-        def quantize(unit):
-            g, gs, first, count = unit
-            codes = keep.tile([P, gs, count], U32, name="codes_%d_%d" % (g, first), align_bytes=64)
-            scales = keep.tile([P, gs, count], U8, name="scales_%d_%d" % (g, first), align_bytes=64)
-            nc.vector.quantize_mx(
-                out=codes[:].rearrange("p g n -> p (g n)").bitcast(FP8X4),
-                scales=scales[:].rearrange("p g n -> p (g n)"),
-                in_=tiles["grouped", unit][:].rearrange("p g n t -> p (g n t)"),
+        def scale_group(j, r0):
+            scale_to_two(scaled[j][:, r0:], w_sb[:, r0:, j * 256 : (j + 1) * 256])
+
+        def sign_group(j, r0):
+            keep_signs(signs[j][:, r0:], scaled[j][:, r0:])
+
+        def regroup(g, j):
+            nc.scalar.activation(
+                out=by_column(grouped[:, j, g]),
+                in_=by_slab(signs[j][:, g * PACK : (g + 1) * PACK]),
+                func=ACT.Copy, scale=half_alpha[:],
             )
-            j = acc_first.index(first)
-            for i in range(gs):
-                nc.tensor.matmul_mx(
-                    out=acc[j][:],
-                    lhsT=x_codes[:, g + i, :].bitcast(FP8X4),
-                    lhsT_scale=x_scales[:, g + i, :],
-                    rhs=codes[:, i, :].bitcast(FP8X4),
-                    rhs_scale=scales[:, i, :],
-                    start=(passes_done[j] == 0),
-                    stop=(passes_done[j] == PASSES - 1),
-                )
-                passes_done[j] += 1
+
+        def quantize(j, g0, g1, src):
+            nc.vector.quantize_mx(
+                out=w_codes[:, j, g0:g1].rearrange("p g n -> p (g n)").bitcast(FP8X4),
+                scales=w_scales[:, j, g0:g1].rearrange("p g n -> p (g n)"),
+                in_=src,
+            )
+
+        def multiply(j, g):
+            nc.tensor.matmul_mx(
+                out=acc[j][:],
+                lhsT=x_codes[:, g, :].bitcast(FP8X4),
+                lhsT_scale=x_scales[:, g, :],
+                rhs=w_codes[:, j, g].bitcast(FP8X4),
+                rhs_scale=w_scales[:, j, g],
+                start=(g == 0),
+                stop=(g == PASSES - 1),
+            )
 
         def add_bias_and_store(j):
-            cols = slice(acc_first[j], acc_first[j] + acc_count[j])
+            cols = slice(j * 256, (j + 1) * 256)
             nc.vector.tensor_tensor(out=out_sb[:, cols], in0=acc[j][:], in1=bias_all[:, cols], op=ALU.add)
             nc.sync.dma_start(out=out[:, cols], in_=out_sb[:, cols])
 
-        early = (0, 1, 0, SPLIT)
-        a = (1, 1, 0, SPLIT)
-        b0 = (0, 2, 512, 256)
-        b1 = (0, 2, 768, 256)
-
-        compare(a)
-        compare(b0)
-        apply_sign(a, 0, 256)
-        apply_sign(a, 256, 512)
-        apply_sign(b0, 0, 256)
-        compare(b1)
-        apply_sign(b1, 0, 256)
-        early_mask = keep.tile([P, SPLIT * PACK], BF16)
+        first_scaled = keep.tile([P, PASSES, 256, PACK], BF16)
+        first_signs = keep.tile([P, PASSES, 256, PACK], BF16)
+        for g in range(PASSES):
+            nc.scalar.activation(
+                out=by_column(first_scaled[:, g]),
+                in_=by_slab(w_sb[:, g * PACK : (g + 1) * PACK, 0:256]),
+                func=ACT.Copy, scale=to_two[:],
+            )
+        nc.scalar.copy(
+            out=x_grouped[:].bitcast(F32), in_=x_t[:].rearrange("p (g u) m -> p g m u", g=PASSES)
+        )
+        scale_group(1, 0)
+        scale_group(2, 0)
+        sign_group(1, 0)
+        regroup(0, 1)
+        regroup(1, 1)
+        scale_group(3, PACK)
+        sign_group(2, 0)
+        regroup(0, 2)
+        regroup(1, 2)
+        scale_to_two(early_scaled[:], early_w[:])
+        sign_group(3, PACK)
+        regroup(1, 3)
+        keep_signs(early_signs[:].rearrange("p n t -> p (n t)"), early_scaled[:].rearrange("p n t -> p (n t)"))
+        keep_signs(first_signs[:].rearrange("p g n t -> p (g n t)"), first_scaled[:].rearrange("p g n t -> p (g n t)"))
         nc.vector.tensor_scalar(
-            out=early_mask[:], in0=abs_grouped[:].rearrange("p n t -> p (n t)"),
-            scalar1=thr, scalar2=twice_alpha, op0=ALU.is_ge, op1=ALU.mult,
+            out=early_wt[:], in0=early_signs[:], scalar1=half_alpha[:], scalar2=None, op0=ALU.mult
+        )
+        nc.vector.tensor_scalar(
+            out=grouped[:, 0], in0=first_signs[:], scalar1=half_alpha[:], scalar2=None, op0=ALU.mult
         )
         nc.vector.quantize_mx(
             out=x_codes[:].rearrange("p g m -> p (g m)").bitcast(FP8X4),
             scales=x_scales[:].rearrange("p g m -> p (g m)"),
             in_=x_grouped[:].rearrange("p g m t -> p (g m t)"),
         )
-        early_wt = new_tile("grouped", early, [P, 1, SPLIT, PACK])
-        nc.vector.tensor_tensor(
-            out=early_wt[:].rearrange("p g n t -> p (g n t)"), in0=early_mask[:],
-            in1=sign_grouped[:].rearrange("p n t -> p (n t)"), op=ALU.mult,
-        )
-        quantize(a)
-        quantize(early)
-        quantize(b0)
-        quantize(b1)
+        quantize(0, 0, 2, grouped[:, 0].rearrange("p g n t -> p (g n t)"))
+        multiply(0, 0)
+        multiply(0, 1)
+        quantize(1, 0, 2, grouped[:, 1].rearrange("p g n t -> p (g n t)"))
+        multiply(1, 0)
+        multiply(1, 1)
+        quantize(3, 0, 1, early_wt[:].rearrange("p n t -> p (n t)"))
+        multiply(3, 0)
         add_bias_and_store(0)
         add_bias_and_store(1)
+        quantize(2, 0, 2, grouped[:, 2].rearrange("p g n t -> p (g n t)"))
+        multiply(2, 0)
+        multiply(2, 1)
+        quantize(3, 1, 2, grouped[:, 3, 1].rearrange("p n t -> p (n t)"))
+        multiply(3, 1)
         add_bias_and_store(2)
+        add_bias_and_store(3)

@@ -25,8 +25,10 @@ KEEP_FROM = 2.0 - 2.0**-8
 MAGNITUDE_BITS = 0x7FFF7FFF
 KEEP_BITS = 0xC000C000 - (1 << 32)
 SPLIT = 640
-LAST_SPLIT = 640
-EARLY = 768
+LAST_SPLIT = 128
+LAST_STT = 640
+EARLY = ((0, 768), (0, 896), (1, 896))
+EARLY_WIDTH = 128
 
 FLOPS = 2 * M * K * N
 
@@ -50,18 +52,22 @@ def tile_ternarydense_s_kernel(tc, x, w, b, out):
         for r in range(SLABS - 1):
             nc.sync.dma_start(out=w_sb[:, r, :], in_=w_rows[r // 2, r % 2])
         last = SLABS - 1
-        for lo, hi in ((0, LAST_SPLIT), (LAST_SPLIT, N)):
+        for lo, hi in ((0, LAST_STT), (LAST_STT, N)):
             nc.sync.dma_start(out=w_sb[:, last, lo:hi], in_=w_rows[last // 2, last % 2, :, lo:hi])
         x_sb = keep.tile([P, K], BF16)
         nc.sync.dma_start(out=x_sb[:], in_=x)
         bias_all = keep.tile([P, N], BF16)
         nc.sync.dma_start(out=bias_all[:], in_=b.partition_broadcast(P))
 
-        scalar_sums = keep.tile([P, SLABS + 8], F32)
-        w_abs = keep.tile([P, SLABS - 1, SPLIT], BF16)
+        sums = keep.tile([P, SLABS], F32)
+        vector_sums = keep.tile([P, 2], F32)
+        w_abs = keep.tile([P, SLABS, SPLIT], BF16)
         scratch = keep.tile([P, SLABS, N], BF16)
         partial = psum.tile([P, 1], F32)
         total = psum.tile([P, 1], F32)
+
+        def add_to_total(column, start=False, stop=False):
+            nc.tensor.matmul(out=total[:], lhsT=ones[:], rhs=column, start=start, stop=stop)
 
         def by_column(tile):
             return tile.rearrange("p (c i) t -> p c t i", i=4)
@@ -69,40 +75,47 @@ def tile_ternarydense_s_kernel(tc, x, w, b, out):
         def by_slab(tile):
             return tile.rearrange("p t (c i) -> p c t i", i=4)
 
-        early_w = keep.tile([P, N - EARLY, PACK], BF16)
-        blocks = [(r, c) for r in range(last) for c in range(SPLIT // P)]
+        early_w = keep.tile([P, len(EARLY), EARLY_WIDTH, PACK], BF16)
+
+        def regroup_early(i):
+            g, first = EARLY[i]
+            nc.vector.tensor_copy(
+                out=by_column(early_w[:, i]),
+                in_=by_slab(w_sb[:, g * PACK : (g + 1) * PACK, first : first + EARLY_WIDTH]),
+            )
+
         for r in range(SLABS):
             split = SPLIT if r < last else LAST_SPLIT
+            scalar_from = SPLIT if r < last else LAST_STT
             nc.scalar.activation(
-                out=scratch[:, r, split:N], in_=w_sb[:, r, split:N], func=ACT.Abs,
-                accum_out=scalar_sums[:, r : r + 1],
+                out=scratch[:, r, scalar_from:N], in_=w_sb[:, r, scalar_from:N], func=ACT.Abs,
+                accum_out=sums[:, r : r + 1],
             )
-            if r == last:
-                nc.vector.scalar_tensor_tensor(
-                    out=scratch[:, r, 0:split], in0=w_sb[:, r, 0:split], scalar=-1.0,
-                    in1=w_sb[:, r, 0:split], op0=ALU.mult, op1=ALU.max,
-                    accum_out=scalar_sums[:, SLABS + 1 : SLABS + 2],
-                )
-                continue
             nc.vector.tensor_scalar(
-                out=w_abs[:, r, :].bitcast(I32), in0=w_sb[:, r, 0:SPLIT].bitcast(I32),
+                out=w_abs[:, r, 0:split].bitcast(I32), in0=w_sb[:, r, 0:split].bitcast(I32),
                 scalar1=MAGNITUDE_BITS, scalar2=None, op0=ALU.bitwise_and,
             )
-            for c in range(SPLIT // P):
+            for c in range(split // P):
                 nc.tensor.matmul(
                     out=partial[:], lhsT=w_abs[:, r, c * P : (c + 1) * P], rhs=one_col[:],
-                    start=((r, c) == blocks[0]), stop=((r, c) == blocks[-1]),
+                    start=(r == 0 and c == 0), stop=(r == last and c == split // P - 1),
                 )
+            if r >= 2:
+                add_to_total(sums[:, r - 2 : r - 1], start=(r == 2))
             if r == PACK - 1:
-                nc.vector.tensor_copy(
-                    out=by_column(early_w[:]), in_=by_slab(w_sb[:, 0:PACK, EARLY:N])
-                )
-        nc.vector.tensor_copy(out=scalar_sums[:, SLABS : SLABS + 1], in_=partial[:])
-        row_sum = keep.tile([P, 1], F32)
-        nc.vector.tensor_reduce(
-            out=row_sum[:], in_=scalar_sums[:, 0 : SLABS + 2], axis=AXIS_X, op=ALU.add
+                regroup_early(0)
+                regroup_early(1)
+        nc.vector.scalar_tensor_tensor(
+            out=scratch[:, last, LAST_SPLIT:LAST_STT], in0=w_sb[:, last, LAST_SPLIT:LAST_STT], scalar=-1.0,
+            in1=w_sb[:, last, LAST_SPLIT:LAST_STT], op0=ALU.mult, op1=ALU.max,
+            accum_out=vector_sums[:, 0:1],
         )
-        nc.tensor.matmul(out=total[:], lhsT=ones[:], rhs=row_sum[:], start=True, stop=True)
+        nc.vector.tensor_copy(out=vector_sums[:, 1:2], in_=partial[:])
+        add_to_total(sums[:, last - 1 : last])
+        add_to_total(vector_sums[:, 0:1])
+        add_to_total(sums[:, last : last + 1])
+        add_to_total(vector_sums[:, 1:2], stop=True)
+        regroup_early(2)
         inverse = keep.tile([P, 1], F32)
         nc.vector.reciprocal(out=inverse[:], in_=total[:])
         to_two = keep.tile([P, 1], F32)
@@ -123,22 +136,33 @@ def tile_ternarydense_s_kernel(tc, x, w, b, out):
         x_codes = keep.tile([P, PASSES, M], U32, align_bytes=64)
         x_scales = keep.tile([P, PASSES, M], U8, align_bytes=64)
 
-        acc_first = (0, 256, 512, 768)
-        acc = [psum.tile([P, 256], F32, name="acc_%d" % first) for first in acc_first]
-        passes_done = [0] * len(acc)
+        groups = ((0, 256), (256, 256), (512, 256), (768, 128), (896, 128))
+        acc = [psum.tile([P, count], F32, name="acc_%d" % first) for first, count in groups]
         out_sb = keep.tile([P, N], F32)
-        scaled = [keep.tile([P, SLABS, 256], BF16, name="scaled_%d" % first) for first in acc_first]
-        signs = [keep.tile([P, SLABS, 256], BF16, name="signs_%d" % first) for first in acc_first]
-        grouped = keep.tile([P, N // 256, PASSES, 256, PACK], BF16, align_bytes=64)
-        early_scaled = keep.tile([P, N - EARLY, PACK], BF16)
-        early_signs = keep.tile([P, N - EARLY, PACK], BF16)
-        early_wt = keep.tile([P, N - EARLY, PACK], BF16, align_bytes=64)
-        w_codes = keep.tile([P, N // 256, PASSES, 256], U32, align_bytes=64)
-        w_scales = keep.tile([P, N // 256, PASSES, 256], U8, align_bytes=64)
+        scaled = [keep.tile([P, SLABS, count], BF16, name="scaled_%d" % first) for first, count in groups]
+        signs = [keep.tile([P, SLABS, count], BF16, name="signs_%d" % first) for first, count in groups]
+        grouped = [
+            keep.tile([P, PASSES, count, PACK], BF16, name="grouped_%d" % first, align_bytes=64)
+            for first, count in groups
+        ]
+        first_scaled = keep.tile([P, PASSES, 256, PACK], BF16)
+        first_signs = keep.tile([P, PASSES, 256, PACK], BF16)
+        early_scaled = keep.tile([P, len(EARLY), EARLY_WIDTH, PACK], BF16)
+        early_signs = keep.tile([P, len(EARLY), EARLY_WIDTH, PACK], BF16)
+        early_wt = keep.tile([P, len(EARLY), EARLY_WIDTH, PACK], BF16, align_bytes=64)
+        w_codes = [
+            keep.tile([P, PASSES, count], U32, name="codes_%d" % first, align_bytes=64)
+            for first, count in groups
+        ]
+        w_scales = [
+            keep.tile([P, PASSES, count], U8, name="scales_%d" % first, align_bytes=64)
+            for first, count in groups
+        ]
 
         def scale_to_two(dst, src):
             nc.vector.tensor_scalar(
-                out=dst, in0=src, scalar1=to_two[:], scalar2=None, op0=ALU.mult
+                out=dst, in0=src, scalar1=inverse[:], scalar2=KEEP_FROM / (THRESHOLD_FACTOR * MEAN),
+                op0=ALU.mult, op1=ALU.mult,
             )
 
         def keep_signs(dst, src):
@@ -147,44 +171,46 @@ def tile_ternarydense_s_kernel(tc, x, w, b, out):
                 op0=ALU.bitwise_and,
             )
 
+        def times_half_alpha(dst, src):
+            nc.vector.tensor_scalar(out=dst, in0=src, scalar1=half_alpha[:], scalar2=None, op0=ALU.mult)
+
         def scale_group(j, r0):
-            scale_to_two(scaled[j][:, r0:], w_sb[:, r0:, j * 256 : (j + 1) * 256])
+            first, count = groups[j]
+            scale_to_two(scaled[j][:, r0:], w_sb[:, r0:, first : first + count])
 
         def sign_group(j, r0):
             keep_signs(signs[j][:, r0:], scaled[j][:, r0:])
 
-        def regroup(g, j):
+        def regroup(j, g):
             nc.scalar.activation(
-                out=by_column(grouped[:, j, g]),
+                out=by_column(grouped[j][:, g]),
                 in_=by_slab(signs[j][:, g * PACK : (g + 1) * PACK]),
                 func=ACT.Copy, scale=half_alpha[:],
             )
 
         def quantize(j, g0, g1, src):
             nc.vector.quantize_mx(
-                out=w_codes[:, j, g0:g1].rearrange("p g n -> p (g n)").bitcast(FP8X4),
-                scales=w_scales[:, j, g0:g1].rearrange("p g n -> p (g n)"),
-                in_=src,
+                out=w_codes[j][:, g0:g1].rearrange("p g n -> p (g n)").bitcast(FP8X4),
+                scales=w_scales[j][:, g0:g1].rearrange("p g n -> p (g n)"),
+                in_=src.rearrange("p g n t -> p (g n t)"),
             )
-
-        def multiply(j, g):
-            nc.tensor.matmul_mx(
-                out=acc[j][:],
-                lhsT=x_codes[:, g, :].bitcast(FP8X4),
-                lhsT_scale=x_scales[:, g, :],
-                rhs=w_codes[:, j, g].bitcast(FP8X4),
-                rhs_scale=w_scales[:, j, g],
-                start=(g == 0),
-                stop=(g == PASSES - 1),
-            )
+            for g in range(g0, g1):
+                nc.tensor.matmul_mx(
+                    out=acc[j][:],
+                    lhsT=x_codes[:, g, :].bitcast(FP8X4),
+                    lhsT_scale=x_scales[:, g, :],
+                    rhs=w_codes[j][:, g].bitcast(FP8X4),
+                    rhs_scale=w_scales[j][:, g],
+                    start=(g == 0),
+                    stop=(g == PASSES - 1),
+                )
 
         def add_bias_and_store(j):
-            cols = slice(j * 256, (j + 1) * 256)
+            first, count = groups[j]
+            cols = slice(first, first + count)
             nc.vector.tensor_tensor(out=out_sb[:, cols], in0=acc[j][:], in1=bias_all[:, cols], op=ALU.add)
             nc.sync.dma_start(out=out[:, cols], in_=out_sb[:, cols])
 
-        first_scaled = keep.tile([P, PASSES, 256, PACK], BF16)
-        first_signs = keep.tile([P, PASSES, 256, PACK], BF16)
         for g in range(PASSES):
             nc.scalar.activation(
                 out=by_column(first_scaled[:, g]),
@@ -197,42 +223,32 @@ def tile_ternarydense_s_kernel(tc, x, w, b, out):
         scale_group(1, 0)
         scale_group(2, 0)
         sign_group(1, 0)
-        regroup(0, 1)
+        regroup(1, 0)
         regroup(1, 1)
         scale_group(3, PACK)
         sign_group(2, 0)
-        regroup(0, 2)
-        regroup(1, 2)
+        regroup(2, 0)
+        regroup(2, 1)
         scale_to_two(early_scaled[:], early_w[:])
         sign_group(3, PACK)
-        regroup(1, 3)
-        keep_signs(early_signs[:].rearrange("p n t -> p (n t)"), early_scaled[:].rearrange("p n t -> p (n t)"))
+        regroup(3, 1)
         keep_signs(first_signs[:].rearrange("p g n t -> p (g n t)"), first_scaled[:].rearrange("p g n t -> p (g n t)"))
-        nc.vector.tensor_scalar(
-            out=early_wt[:], in0=early_signs[:], scalar1=half_alpha[:], scalar2=None, op0=ALU.mult
-        )
-        nc.vector.tensor_scalar(
-            out=grouped[:, 0], in0=first_signs[:], scalar1=half_alpha[:], scalar2=None, op0=ALU.mult
-        )
+        keep_signs(early_signs[:].rearrange("p i n t -> p (i n t)"), early_scaled[:].rearrange("p i n t -> p (i n t)"))
+        times_half_alpha(grouped[0][:], first_signs[:])
         nc.vector.quantize_mx(
             out=x_codes[:].rearrange("p g m -> p (g m)").bitcast(FP8X4),
             scales=x_scales[:].rearrange("p g m -> p (g m)"),
             in_=x_grouped[:].rearrange("p g m t -> p (g m t)"),
         )
-        quantize(0, 0, 2, grouped[:, 0].rearrange("p g n t -> p (g n t)"))
-        multiply(0, 0)
-        multiply(0, 1)
-        quantize(1, 0, 2, grouped[:, 1].rearrange("p g n t -> p (g n t)"))
-        multiply(1, 0)
-        multiply(1, 1)
-        quantize(3, 0, 1, early_wt[:].rearrange("p n t -> p (n t)"))
-        multiply(3, 0)
+        quantize(0, 0, 2, grouped[0][:])
+        times_half_alpha(early_wt[:], early_signs[:])
+        quantize(1, 0, 2, grouped[1][:])
         add_bias_and_store(0)
+        quantize(3, 0, 1, early_wt[:, 0:1])
+        quantize(4, 0, 2, early_wt[:, 1:3])
         add_bias_and_store(1)
-        quantize(2, 0, 2, grouped[:, 2].rearrange("p g n t -> p (g n t)"))
-        multiply(2, 0)
-        multiply(2, 1)
-        quantize(3, 1, 2, grouped[:, 3, 1].rearrange("p n t -> p (n t)"))
-        multiply(3, 1)
+        quantize(2, 0, 2, grouped[2][:])
+        quantize(3, 1, 2, grouped[3][:, 1:2])
+        add_bias_and_store(4)
         add_bias_and_store(2)
         add_bias_and_store(3)

@@ -22,13 +22,13 @@ PAIRS = SLABS // 2
 THRESHOLD_FACTOR = 0.7
 MEAN = 1.0 / (K * N)
 KEEP_FROM = 2.0 - 2.0**-8
+PER_SUM = round(THRESHOLD_FACTOR * MEAN / KEEP_FROM * 2**45) / 2**45
 MAGNITUDE_BITS = 0x7FFF7FFF
 KEEP_BITS = 0xC000C000 - (1 << 32)
 SPLIT = 640
-LAST_SPLIT = 128
-LAST_STT = 640
-EARLY = ((0, 768), (0, 896), (1, 896))
-EARLY_WIDTH = 128
+LAST_SPLIT = 256
+LAST_STT = 576
+EARLY = 768
 
 FLOPS = 2 * M * K * N
 
@@ -40,8 +40,8 @@ def tile_ternarydense_s_kernel(tc, x, w, b, out):
         psum = stack.enter_context(tc.psum_pool(name="psum", bufs=1))
         stack.enter_context(tc.manual_schedule())
 
-        ones = keep.tile([P, P], F32)
-        nc.vector.memset(ones[:], 1.0)
+        per_sum = keep.tile([P, P], F32)
+        nc.vector.memset(per_sum[:], PER_SUM)
         one_col = keep.tile([P, 1], BF16)
         nc.vector.memset(one_col[:], 1.0)
         ident = keep.tile([P, P], F32)
@@ -52,22 +52,18 @@ def tile_ternarydense_s_kernel(tc, x, w, b, out):
         for r in range(SLABS - 1):
             nc.sync.dma_start(out=w_sb[:, r, :], in_=w_rows[r // 2, r % 2])
         last = SLABS - 1
-        for lo, hi in ((0, LAST_STT), (LAST_STT, N)):
+        for lo, hi in ((LAST_STT, N), (0, LAST_SPLIT), (LAST_SPLIT, LAST_STT)):
             nc.sync.dma_start(out=w_sb[:, last, lo:hi], in_=w_rows[last // 2, last % 2, :, lo:hi])
         x_sb = keep.tile([P, K], BF16)
         nc.sync.dma_start(out=x_sb[:], in_=x)
         bias_all = keep.tile([P, N], BF16)
         nc.sync.dma_start(out=bias_all[:], in_=b.partition_broadcast(P))
 
-        sums = keep.tile([P, SLABS], F32)
-        vector_sums = keep.tile([P, 2], F32)
+        sums = keep.tile([P, SLABS + 2], F32)
         w_abs = keep.tile([P, SLABS, SPLIT], BF16)
         scratch = keep.tile([P, SLABS, N], BF16)
         partial = psum.tile([P, 1], F32)
         total = psum.tile([P, 1], F32)
-
-        def add_to_total(column, start=False, stop=False):
-            nc.tensor.matmul(out=total[:], lhsT=ones[:], rhs=column, start=start, stop=stop)
 
         def by_column(tile):
             return tile.rearrange("p (c i) t -> p c t i", i=4)
@@ -75,13 +71,11 @@ def tile_ternarydense_s_kernel(tc, x, w, b, out):
         def by_slab(tile):
             return tile.rearrange("p t (c i) -> p c t i", i=4)
 
-        early_w = keep.tile([P, len(EARLY), EARLY_WIDTH, PACK], BF16)
+        early_w = keep.tile([P, PASSES, N - EARLY, PACK], BF16)
 
-        def regroup_early(i):
-            g, first = EARLY[i]
+        def regroup_early(g):
             nc.vector.tensor_copy(
-                out=by_column(early_w[:, i]),
-                in_=by_slab(w_sb[:, g * PACK : (g + 1) * PACK, first : first + EARLY_WIDTH]),
+                out=by_column(early_w[:, g]), in_=by_slab(w_sb[:, g * PACK : (g + 1) * PACK, EARLY:N])
             )
 
         for r in range(SLABS):
@@ -100,32 +94,23 @@ def tile_ternarydense_s_kernel(tc, x, w, b, out):
                     out=partial[:], lhsT=w_abs[:, r, c * P : (c + 1) * P], rhs=one_col[:],
                     start=(r == 0 and c == 0), stop=(r == last and c == split // P - 1),
                 )
-            if r >= 2:
-                add_to_total(sums[:, r - 2 : r - 1], start=(r == 2))
             if r == PACK - 1:
                 regroup_early(0)
-                regroup_early(1)
         nc.vector.scalar_tensor_tensor(
             out=scratch[:, last, LAST_SPLIT:LAST_STT], in0=w_sb[:, last, LAST_SPLIT:LAST_STT], scalar=-1.0,
             in1=w_sb[:, last, LAST_SPLIT:LAST_STT], op0=ALU.mult, op1=ALU.max,
-            accum_out=vector_sums[:, 0:1],
+            accum_out=sums[:, SLABS : SLABS + 1],
         )
-        nc.vector.tensor_copy(out=vector_sums[:, 1:2], in_=partial[:])
-        add_to_total(sums[:, last - 1 : last])
-        add_to_total(vector_sums[:, 0:1])
-        add_to_total(sums[:, last : last + 1])
-        add_to_total(vector_sums[:, 1:2], stop=True)
-        regroup_early(2)
-        inverse = keep.tile([P, 1], F32)
-        nc.vector.reciprocal(out=inverse[:], in_=total[:])
+        nc.vector.tensor_copy(out=sums[:, SLABS + 1 : SLABS + 2], in_=partial[:])
+        row_sum = keep.tile([P, 1], F32)
+        nc.vector.tensor_reduce(out=row_sum[:], in_=sums[:], axis=AXIS_X, op=ALU.add)
+        nc.tensor.matmul(out=total[:], lhsT=per_sum[:], rhs=row_sum[:], start=True, stop=True)
+        regroup_early(1)
         to_two = keep.tile([P, 1], F32)
-        nc.vector.tensor_scalar(
-            out=to_two[:], in0=inverse[:], scalar1=KEEP_FROM / (THRESHOLD_FACTOR * MEAN), scalar2=None,
-            op0=ALU.mult,
-        )
+        nc.vector.reciprocal(out=to_two[:], in_=total[:])
         half_alpha = keep.tile([P, 1], F32)
         nc.vector.tensor_scalar(
-            out=half_alpha[:], in0=total[:], scalar1=MEAN / 2, scalar2=None, op0=ALU.mult
+            out=half_alpha[:], in0=total[:], scalar1=MEAN / 2 / PER_SUM, scalar2=None, op0=ALU.mult
         )
 
         x_words = x_sb[:].bitcast(F32)
@@ -136,7 +121,7 @@ def tile_ternarydense_s_kernel(tc, x, w, b, out):
         x_codes = keep.tile([P, PASSES, M], U32, align_bytes=64)
         x_scales = keep.tile([P, PASSES, M], U8, align_bytes=64)
 
-        groups = ((0, 256), (256, 256), (512, 256), (768, 128), (896, 128))
+        groups = ((0, 256), (256, 256), (512, 256), (768, 256))
         acc = [psum.tile([P, count], F32, name="acc_%d" % first) for first, count in groups]
         out_sb = keep.tile([P, N], F32)
         scaled = [keep.tile([P, SLABS, count], BF16, name="scaled_%d" % first) for first, count in groups]
@@ -147,9 +132,9 @@ def tile_ternarydense_s_kernel(tc, x, w, b, out):
         ]
         first_scaled = keep.tile([P, PASSES, 256, PACK], BF16)
         first_signs = keep.tile([P, PASSES, 256, PACK], BF16)
-        early_scaled = keep.tile([P, len(EARLY), EARLY_WIDTH, PACK], BF16)
-        early_signs = keep.tile([P, len(EARLY), EARLY_WIDTH, PACK], BF16)
-        early_wt = keep.tile([P, len(EARLY), EARLY_WIDTH, PACK], BF16, align_bytes=64)
+        early_scaled = keep.tile([P, PASSES, N - EARLY, PACK], BF16)
+        early_signs = keep.tile([P, PASSES, N - EARLY, PACK], BF16)
+        early_wt = keep.tile([P, PASSES, N - EARLY, PACK], BF16, align_bytes=64)
         w_codes = [
             keep.tile([P, PASSES, count], U32, name="codes_%d" % first, align_bytes=64)
             for first, count in groups
@@ -161,8 +146,7 @@ def tile_ternarydense_s_kernel(tc, x, w, b, out):
 
         def scale_to_two(dst, src):
             nc.vector.tensor_scalar(
-                out=dst, in0=src, scalar1=inverse[:], scalar2=KEEP_FROM / (THRESHOLD_FACTOR * MEAN),
-                op0=ALU.mult, op1=ALU.mult,
+                out=dst, in0=src, scalar1=to_two[:], scalar2=None, op0=ALU.mult
             )
 
         def keep_signs(dst, src):
@@ -174,12 +158,15 @@ def tile_ternarydense_s_kernel(tc, x, w, b, out):
         def times_half_alpha(dst, src):
             nc.vector.tensor_scalar(out=dst, in0=src, scalar1=half_alpha[:], scalar2=None, op0=ALU.mult)
 
-        def scale_group(j, r0):
+        def scale_group(j):
             first, count = groups[j]
-            scale_to_two(scaled[j][:, r0:], w_sb[:, r0:, first : first + count])
+            scale_to_two(scaled[j][:], w_sb[:, :, first : first + count])
 
-        def sign_group(j, r0):
-            keep_signs(signs[j][:, r0:], scaled[j][:, r0:])
+        def sign_group(j):
+            keep_signs(signs[j][:], scaled[j][:])
+
+        def flat(tile):
+            return tile[:].rearrange("p g n t -> p (g n t)")
 
         def regroup(j, g):
             nc.scalar.activation(
@@ -188,13 +175,13 @@ def tile_ternarydense_s_kernel(tc, x, w, b, out):
                 func=ACT.Copy, scale=half_alpha[:],
             )
 
-        def quantize(j, g0, g1, src):
+        def quantize(j, src):
             nc.vector.quantize_mx(
-                out=w_codes[j][:, g0:g1].rearrange("p g n -> p (g n)").bitcast(FP8X4),
-                scales=w_scales[j][:, g0:g1].rearrange("p g n -> p (g n)"),
-                in_=src.rearrange("p g n t -> p (g n t)"),
+                out=w_codes[j][:].rearrange("p g n -> p (g n)").bitcast(FP8X4),
+                scales=w_scales[j][:].rearrange("p g n -> p (g n)"),
+                in_=flat(src),
             )
-            for g in range(g0, g1):
+            for g in range(PASSES):
                 nc.tensor.matmul_mx(
                     out=acc[j][:],
                     lhsT=x_codes[:, g, :].bitcast(FP8X4),
@@ -220,35 +207,29 @@ def tile_ternarydense_s_kernel(tc, x, w, b, out):
         nc.scalar.copy(
             out=x_grouped[:].bitcast(F32), in_=x_t[:].rearrange("p (g u) m -> p g m u", g=PASSES)
         )
-        scale_group(1, 0)
-        scale_group(2, 0)
-        sign_group(1, 0)
+        scale_group(1)
+        scale_group(2)
+        sign_group(1)
         regroup(1, 0)
         regroup(1, 1)
-        scale_group(3, PACK)
-        sign_group(2, 0)
+        sign_group(2)
         regroup(2, 0)
         regroup(2, 1)
         scale_to_two(early_scaled[:], early_w[:])
-        sign_group(3, PACK)
-        regroup(3, 1)
-        keep_signs(first_signs[:].rearrange("p g n t -> p (g n t)"), first_scaled[:].rearrange("p g n t -> p (g n t)"))
-        keep_signs(early_signs[:].rearrange("p i n t -> p (i n t)"), early_scaled[:].rearrange("p i n t -> p (i n t)"))
+        keep_signs(flat(first_signs), flat(first_scaled))
+        keep_signs(flat(early_signs), flat(early_scaled))
         times_half_alpha(grouped[0][:], first_signs[:])
+        times_half_alpha(early_wt[:], early_signs[:])
         nc.vector.quantize_mx(
             out=x_codes[:].rearrange("p g m -> p (g m)").bitcast(FP8X4),
             scales=x_scales[:].rearrange("p g m -> p (g m)"),
             in_=x_grouped[:].rearrange("p g m t -> p (g m t)"),
         )
-        quantize(0, 0, 2, grouped[0][:])
-        times_half_alpha(early_wt[:], early_signs[:])
-        quantize(1, 0, 2, grouped[1][:])
+        quantize(0, grouped[0])
+        quantize(3, early_wt)
+        quantize(1, grouped[1])
         add_bias_and_store(0)
-        quantize(3, 0, 1, early_wt[:, 0:1])
-        quantize(4, 0, 2, early_wt[:, 1:3])
-        add_bias_and_store(1)
-        quantize(2, 0, 2, grouped[2][:])
-        quantize(3, 1, 2, grouped[3][:, 1:2])
-        add_bias_and_store(4)
-        add_bias_and_store(2)
+        quantize(2, grouped[2])
         add_bias_and_store(3)
+        add_bias_and_store(1)
+        add_bias_and_store(2)

from contextlib import ExitStack

import concourse.mybir as mybir
from concourse.masks import make_identity

BF16 = mybir.dt.bfloat16
F32 = mybir.dt.float32
I32 = mybir.dt.int32
U32 = mybir.dt.uint32
U8 = mybir.dt.uint8
FP8X4 = mybir.dt.float8_e4m3fn_x4
ALU = mybir.AluOpType
ACT = mybir.ActivationFunctionType
AXIS_X = mybir.AxisListType.X

P = 128
PACK = 4
M, K, N = 128, 1024, 1024
PASSES = K // (P * PACK)
SLABS = K // P
PAIRS = SLABS // 2
THRESHOLD_FACTOR = 0.7
MEAN = 1.0 / (K * N)
KEEP_FROM = 2.0 - 2.0**-8
PER_SUM = round(THRESHOLD_FACTOR * MEAN / KEEP_FROM * 2**45) / 2**45
MAGNITUDE_BITS = 0x7FFF7FFF
KEEP_BITS = 0xC000C000 - (1 << 32)
SPLIT = 640
LAST_SPLIT = 256
LAST_STT = 576
EARLY = 768

FLOPS = 2 * M * K * N


def tile_ternarydense_s_kernel(tc, x, w, b, out):
    nc = tc.nc
    with ExitStack() as stack:
        keep = stack.enter_context(tc.tile_pool(name="keep", bufs=1))
        psum = stack.enter_context(tc.psum_pool(name="psum", bufs=1))
        stack.enter_context(tc.manual_schedule())

        per_sum = keep.tile([P, P], F32)
        nc.vector.memset(per_sum[:], PER_SUM)
        one_col = keep.tile([P, 1], BF16)
        nc.vector.memset(one_col[:], 1.0)
        ident = keep.tile([P, P], F32)
        make_identity(nc, ident[:])

        w_sb = keep.tile([P, SLABS, N], BF16)
        w_rows = w.rearrange("(s p e) n -> s e p n", p=P, e=2)
        for r in range(SLABS - 1):
            nc.sync.dma_start(out=w_sb[:, r, :], in_=w_rows[r // 2, r % 2])
        last = SLABS - 1
        for lo, hi in ((LAST_STT, N), (0, LAST_SPLIT), (LAST_SPLIT, LAST_STT)):
            nc.sync.dma_start(out=w_sb[:, last, lo:hi], in_=w_rows[last // 2, last % 2, :, lo:hi])
        x_sb = keep.tile([P, K], BF16)
        nc.sync.dma_start(out=x_sb[:], in_=x)
        bias_all = keep.tile([P, N], BF16)
        nc.sync.dma_start(out=bias_all[:], in_=b.partition_broadcast(P))

        sums = keep.tile([P, SLABS + 2], F32)
        w_abs = keep.tile([P, SLABS, SPLIT], BF16)
        scratch = keep.tile([P, SLABS, N], BF16)
        partial = psum.tile([P, 1], F32)
        total = psum.tile([P, 1], F32)

        def by_column(tile):
            return tile.rearrange("p (c i) t -> p c t i", i=4)

        def by_slab(tile):
            return tile.rearrange("p t (c i) -> p c t i", i=4)

        early_w = keep.tile([P, PASSES, N - EARLY, PACK], BF16)

        def regroup_early(g):
            nc.vector.tensor_copy(
                out=by_column(early_w[:, g]), in_=by_slab(w_sb[:, g * PACK : (g + 1) * PACK, EARLY:N])
            )

        for r in range(SLABS):
            split = SPLIT if r < last else LAST_SPLIT
            scalar_from = SPLIT if r < last else LAST_STT
            nc.scalar.activation(
                out=scratch[:, r, scalar_from:N], in_=w_sb[:, r, scalar_from:N], func=ACT.Abs,
                accum_out=sums[:, r : r + 1],
            )
            nc.vector.tensor_scalar(
                out=w_abs[:, r, 0:split].bitcast(I32), in0=w_sb[:, r, 0:split].bitcast(I32),
                scalar1=MAGNITUDE_BITS, scalar2=None, op0=ALU.bitwise_and,
            )
            for c in range(split // P):
                nc.tensor.matmul(
                    out=partial[:], lhsT=w_abs[:, r, c * P : (c + 1) * P], rhs=one_col[:],
                    start=(r == 0 and c == 0), stop=(r == last and c == split // P - 1),
                )
            if r == PACK - 1:
                regroup_early(0)
        nc.vector.scalar_tensor_tensor(
            out=scratch[:, last, LAST_SPLIT:LAST_STT], in0=w_sb[:, last, LAST_SPLIT:LAST_STT], scalar=-1.0,
            in1=w_sb[:, last, LAST_SPLIT:LAST_STT], op0=ALU.mult, op1=ALU.max,
            accum_out=sums[:, SLABS : SLABS + 1],
        )
        nc.vector.tensor_copy(out=sums[:, SLABS + 1 : SLABS + 2], in_=partial[:])
        row_sum = keep.tile([P, 1], F32)
        nc.vector.tensor_reduce(out=row_sum[:], in_=sums[:], axis=AXIS_X, op=ALU.add)
        nc.tensor.matmul(out=total[:], lhsT=per_sum[:], rhs=row_sum[:], start=True, stop=True)
        regroup_early(1)
        to_two = keep.tile([P, 1], F32)
        nc.vector.reciprocal(out=to_two[:], in_=total[:])
        half_alpha = keep.tile([P, 1], F32)
        nc.vector.tensor_scalar(
            out=half_alpha[:], in0=total[:], scalar1=MEAN / 2 / PER_SUM, scalar2=None, op0=ALU.mult
        )

        x_words = x_sb[:].bitcast(F32)
        x_t = psum.tile([P, PAIRS, M], F32)
        for s in range(PAIRS):
            nc.tensor.transpose(x_t[:, s, :], x_words[:, s * P : (s + 1) * P], ident[:])
        x_grouped = keep.tile([P, PASSES, M, PACK], BF16, align_bytes=64)
        x_codes = keep.tile([P, PASSES, M], U32, align_bytes=64)
        x_scales = keep.tile([P, PASSES, M], U8, align_bytes=64)

        groups = ((0, 256), (256, 256), (512, 256), (768, 256))
        acc = [psum.tile([P, count], F32, name="acc_%d" % first) for first, count in groups]
        out_sb = keep.tile([P, N], F32)
        scaled = [keep.tile([P, SLABS, count], BF16, name="scaled_%d" % first) for first, count in groups]
        signs = [keep.tile([P, SLABS, count], BF16, name="signs_%d" % first) for first, count in groups]
        grouped = [
            keep.tile([P, PASSES, count, PACK], BF16, name="grouped_%d" % first, align_bytes=64)
            for first, count in groups
        ]
        first_scaled = keep.tile([P, PASSES, 256, PACK], BF16)
        first_signs = keep.tile([P, PASSES, 256, PACK], BF16)
        early_scaled = keep.tile([P, PASSES, N - EARLY, PACK], BF16)
        early_signs = keep.tile([P, PASSES, N - EARLY, PACK], BF16)
        early_wt = keep.tile([P, PASSES, N - EARLY, PACK], BF16, align_bytes=64)
        w_codes = [
            keep.tile([P, PASSES, count], U32, name="codes_%d" % first, align_bytes=64)
            for first, count in groups
        ]
        w_scales = [
            keep.tile([P, PASSES, count], U8, name="scales_%d" % first, align_bytes=64)
            for first, count in groups
        ]

        def scale_to_two(dst, src):
            nc.vector.tensor_scalar(
                out=dst, in0=src, scalar1=to_two[:], scalar2=None, op0=ALU.mult
            )

        def keep_signs(dst, src):
            nc.vector.tensor_scalar(
                out=dst.bitcast(I32), in0=src.bitcast(I32), scalar1=KEEP_BITS, scalar2=None,
                op0=ALU.bitwise_and,
            )

        def times_half_alpha(dst, src):
            nc.vector.tensor_scalar(out=dst, in0=src, scalar1=half_alpha[:], scalar2=None, op0=ALU.mult)

        def scale_group(j):
            first, count = groups[j]
            scale_to_two(scaled[j][:], w_sb[:, :, first : first + count])

        def sign_group(j):
            keep_signs(signs[j][:], scaled[j][:])

        def flat(tile):
            return tile[:].rearrange("p g n t -> p (g n t)")

        def regroup(j, g):
            nc.scalar.activation(
                out=by_column(grouped[j][:, g]),
                in_=by_slab(signs[j][:, g * PACK : (g + 1) * PACK]),
                func=ACT.Copy, scale=half_alpha[:],
            )

        def quantize(j, src):
            nc.vector.quantize_mx(
                out=w_codes[j][:].rearrange("p g n -> p (g n)").bitcast(FP8X4),
                scales=w_scales[j][:].rearrange("p g n -> p (g n)"),
                in_=flat(src),
            )
            for g in range(PASSES):
                nc.tensor.matmul_mx(
                    out=acc[j][:],
                    lhsT=x_codes[:, g, :].bitcast(FP8X4),
                    lhsT_scale=x_scales[:, g, :],
                    rhs=w_codes[j][:, g].bitcast(FP8X4),
                    rhs_scale=w_scales[j][:, g],
                    start=(g == 0),
                    stop=(g == PASSES - 1),
                )

        def add_bias_and_store(j):
            first, count = groups[j]
            cols = slice(first, first + count)
            nc.vector.tensor_tensor(out=out_sb[:, cols], in0=acc[j][:], in1=bias_all[:, cols], op=ALU.add)
            nc.sync.dma_start(out=out[:, cols], in_=out_sb[:, cols])

        for g in range(PASSES):
            nc.scalar.activation(
                out=by_column(first_scaled[:, g]),
                in_=by_slab(w_sb[:, g * PACK : (g + 1) * PACK, 0:256]),
                func=ACT.Copy, scale=to_two[:],
            )
        nc.scalar.copy(
            out=x_grouped[:].bitcast(F32), in_=x_t[:].rearrange("p (g u) m -> p g m u", g=PASSES)
        )
        scale_group(1)
        scale_group(2)
        sign_group(1)
        regroup(1, 0)
        regroup(1, 1)
        sign_group(2)
        regroup(2, 0)
        regroup(2, 1)
        scale_to_two(early_scaled[:], early_w[:])
        keep_signs(flat(first_signs), flat(first_scaled))
        keep_signs(flat(early_signs), flat(early_scaled))
        times_half_alpha(grouped[0][:], first_signs[:])
        times_half_alpha(early_wt[:], early_signs[:])
        nc.vector.quantize_mx(
            out=x_codes[:].rearrange("p g m -> p (g m)").bitcast(FP8X4),
            scales=x_scales[:].rearrange("p g m -> p (g m)"),
            in_=x_grouped[:].rearrange("p g m t -> p (g m t)"),
        )
        quantize(0, grouped[0])
        quantize(3, early_wt)
        quantize(1, grouped[1])
        add_bias_and_store(0)
        quantize(2, grouped[2])
        add_bias_and_store(3)
        add_bias_and_store(1)
        add_bias_and_store(2)
